import numpy as np
import ml_dtypes


def mxq(x, axis, fmt="e4m3"):
    dtype, down = {"e4m3": (ml_dtypes.float8_e4m3fn, 7), "e5m2": (ml_dtypes.float8_e5m2, 14)}[fmt]
    v = np.moveaxis(np.asarray(x, np.float32).astype(ml_dtypes.bfloat16).astype(np.float64), axis, -1)
    blocks = v.reshape(v.shape[:-1] + (-1, 32))
    amax = np.abs(blocks).max(-1, keepdims=True)
    byte = np.maximum(np.where(amax > 0, np.frexp(amax)[1] - 1 + 127, 0) - down, 1)
    scale = np.exp2(byte - 127.0)
    codes = (blocks / scale).astype(np.float32).astype(dtype).astype(np.float64)
    return np.moveaxis((codes * scale).reshape(v.shape), -1, axis)


WIDE = False


def mx_kscale(k):
    if not WIDE:
        return np.ones(k)
    levels = np.array([10, -10, 5, -5, 0])
    a = np.random.permutation(np.resize(levels, k // 512 * 4)).reshape(k // 512, 4)
    idx = np.arange(k)
    return np.exp2(a[idx // 512, idx % 128 // 32])


BF16 = ml_dtypes.bfloat16


def bf(x):
    return np.asarray(x, np.float32).astype(BF16)


def f64(x):
    return np.asarray(x).astype(np.float64)


B, H, S, D, W = 8, 1, 512, 256, 128
NEG = -1e9
BLK = 32


def key_factors():
    f = np.array(mx_kscale(S), dtype=np.float64)
    hi, lo = f.max(), f.min()
    lev = f.reshape(-1, BLK)[:, 0].copy()
    lev[0::4] = hi
    lev[2::4] = lo
    return np.repeat(lev, BLK) / hi


def swa_mask(s):
    i = np.arange(S)[:, None]
    j = np.arange(S)[None, :]
    allowed = (j <= i) & (j > i - W)
    return np.where(allowed, 0.1 * np.random.standard_normal((S, S)) + np.log(s)[None, :], NEG)[None, None]


def setup_inputs():
    a = np.sqrt(2.0 / np.sqrt(D))
    s = key_factors()
    return {"q": bf(np.random.standard_normal((B, H, S, D)) * a), "k": bf(np.random.standard_normal((B, H, S, D)) * a),
            "v": bf(np.random.standard_normal((B, H, S, D)) / s[:, None]), "mask": bf(swa_mask(s))}


def reference(q, k, v, mask):
    a = f64(q) @ f64(k).transpose(0, 1, 3, 2) + f64(mask)
    e = np.exp(a - a.max(-1, keepdims=True))
    return (mxq(e, 3, "e4m3") @ mxq(f64(v), 2, "e4m3")) / e.sum(-1, keepdims=True)

@@ -1,0 +1,226 @@
+from contextlib import ExitStack
+
+import concourse.mybir as mybir
+from concourse.masks import make_identity
+
+F32 = mybir.dt.float32
+BF16 = mybir.dt.bfloat16
+U32 = mybir.dt.uint32
+U8 = mybir.dt.uint8
+FP8X4 = mybir.dt.float8_e4m3fn_x4
+ACT = mybir.ActivationFunctionType
+ALU = mybir.AluOpType
+AX = mybir.AxisListType
+
+B, S, D = 8, 512, 256
+P = 128
+FLOPS = 4 * B * S * S * D
+
+
+def tile_manualblock_t_kernel(tc, q, k, v, mask, out):
+    nc = tc.nc
+    qf = q.flatten_outer_dims()
+    kf = k.flatten_outer_dims()
+    vf = v.flatten_outer_dims()
+    mf = mask.flatten_outer_dims()
+    of = out.flatten_outer_dims()
+
+    with ExitStack() as ctx:
+        const = ctx.enter_context(tc.tile_pool(name="const", bufs=1))
+        raw = ctx.enter_context(tc.tile_pool(name="raw", bufs=B))
+        tsb = ctx.enter_context(tc.tile_pool(name="tsb", bufs=3))
+        vq = ctx.enter_context(tc.tile_pool(name="vq", bufs=4))
+        unit = ctx.enter_context(tc.tile_pool(name="unit", bufs=3))
+        small = ctx.enter_context(tc.tile_pool(name="small", bufs=6))
+        ps_t = ctx.enter_context(tc.psum_pool(name="ps_t", bufs=2))
+        ps_s = ctx.enter_context(tc.psum_pool(name="ps_s", bufs=2))
+        ps_e = ctx.enter_context(tc.psum_pool(name="ps_e", bufs=1))
+        ps_o = ctx.enter_context(tc.psum_pool(name="ps_o", bufs=2))
+
+        kraw, qraw, vraw = [], [], []
+        mask_sb = const.tile([P, 4, 256], BF16, name="mask_sb")
+        for b in range(B):
+            rows = slice(b * S, (b + 1) * S)
+            kr = raw.tile([P, 1024], BF16, name="kraw")
+            nc.sync.dma_start(out=kr[:], in_=kf[rows, :].rearrange("(p t) d -> p (t d)", t=4))
+            qr = raw.tile([P, 1024], BF16, name="qraw")
+            nc.sync.dma_start(out=qr[:], in_=qf[rows, :].rearrange("(p t) d -> p (t d)", t=4))
+            vr = raw.tile([P, 4, 256], BF16, name="vraw")
+            nc.sync.dma_start(out=vr[:], in_=vf[rows, :].rearrange("(t p) d -> p t d", p=P))
+            kraw.append(kr)
+            qraw.append(qr)
+            vraw.append(vr)
+        nc.scalar.dma_start(out=mask_sb[:, 0, 0:128], in_=mf[0:128, 0:128])
+        for i in range(1, 4):
+            nc.scalar.dma_start(
+                out=mask_sb[:, i, :], in_=mf[i * P : (i + 1) * P, (i - 1) * P : (i + 1) * P]
+            )
+
+        ident_f = const.tile([P, P], F32, name="ident_f")
+        make_identity(nc, ident_f[:])
+        ident_b = const.tile([P, P], BF16, name="ident_b")
+        make_identity(nc, ident_b[:])
+        zero_b = const.tile([P, P], BF16, name="zero_b")
+        nc.vector.memset(zero_b[:], 0.0)
+        grouped = []
+        for n in range(4):
+            g = const.tile([P, 1056], BF16, name="grouped%d" % n, align_bytes=64)
+            nc.vector.memset(g[:], 0.0)
+            grouped.append(g)
+        et = []
+        for h in range(2):
+            t_ = ps_e.tile([P, 1024], BF16, name="et%d" % h)
+            et.append(t_)
+        nc.tensor.transpose(out=et[0][:, 128:256], in_=zero_b[:], identity=ident_b[:])
+
+        q_t, k_t, v_c, v_s = {}, {}, {}, {}
+        s_ps, e_sb, r_sum, e_c, e_s = {}, {}, {}, {}, {}
+
+        def stage_t(b):
+            for which, src, dst in (("k", kraw[b], k_t), ("q", qraw[b], q_t)):
+                words = src[:].bitcast(F32)
+                tp = ps_t.tile([P, 512], F32, name="tp")
+                for t in range(4):
+                    cols = slice(t * P, (t + 1) * P)
+                    nc.tensor.transpose(out=tp[:, cols], in_=words[:, cols], identity=ident_f[:])
+                sb = tsb.tile([P, 512], F32, name=which + "_t")
+                o_view = sb[:].rearrange("w (p t) -> w p t", t=4)
+                i_view = tp[:].rearrange("w (t p) -> w p t", t=4)
+                if which == "k":
+                    nc.vector.tensor_copy(out=o_view, in_=i_view)
+                else:
+                    nc.scalar.copy(out=o_view, in_=i_view)
+                dst[b] = sb
+
+        def stage_v(b):
+            vg = vq.tile([P, 256, 4], BF16, name="vg", align_bytes=64)
+            nc.vector.tensor_copy(
+                out=vg[:].rearrange("p (c i) t -> p c t i", i=4),
+                in_=vraw[b][:].rearrange("p t (c i) -> p c t i", i=4),
+            )
+            vc = vq.tile([P, 256], U32, name="vc", align_bytes=64)
+            vs = vq.tile([P, 256], U8, name="vs", align_bytes=64)
+            nc.vector.quantize_mx(
+                out=vc[:].bitcast(FP8X4), scales=vs[:], in_=vg[:].rearrange("p d t -> p (d t)")
+            )
+            v_c[b] = vc
+            v_s[b] = vs
+
+        def windows(h):
+            if h == 0:
+                return ((0, 0, 128, 0), (1, 0, 256, 128))
+            return ((2, 128, 256, 0), (3, 256, 256, 256))
+
+        def stage_s(u):
+            b, h = divmod(u, 2)
+            qb = q_t[b][:].bitcast(BF16).rearrange("w (r e) -> w r e", e=2)
+            kb = k_t[b][:].bitcast(BF16).rearrange("w (r e) -> w r e", e=2)
+            sp = ps_s.tile([P, 512], F32, name="sp")
+            for i, k0, nk, c0 in windows(h):
+                dst = sp[:, c0 : c0 + nk]
+                nc.tensor.matmul(
+                    out=dst, lhsT=ident_b[:], rhs=mask_sb[:, i, 0:nk], start=True, stop=False
+                )
+                for e in range(2):
+                    nc.tensor.matmul(
+                        out=dst,
+                        lhsT=qb[:, i * P : (i + 1) * P, e],
+                        rhs=kb[:, k0 : k0 + nk, e],
+                        start=False,
+                        stop=(e == 1),
+                    )
+            negm = small.tile([P, 2], F32, name="negm")
+            if h == 0:
+                for il, (i, k0, nk, c0) in enumerate(windows(h)):
+                    nc.vector.tensor_reduce(
+                        out=negm[:, il : il + 1], in_=sp[:, c0 : c0 + nk], axis=AX.X, op=ALU.max,
+                        negate=True,
+                    )
+            else:
+                nc.vector.tensor_reduce(
+                    out=negm[:], in_=sp[:].rearrange("q (i c) -> q i c", i=2), axis=AX.X,
+                    op=ALU.max, negate=True,
+                )
+            eb = unit.tile([P, 512], BF16, name="eb")
+            rs = small.tile([P, 2], F32, name="rs")
+            for il, (i, k0, nk, c0) in enumerate(windows(h)):
+                nc.scalar.activation(
+                    out=eb[:, c0 : c0 + nk], in_=sp[:, c0 : c0 + nk], func=ACT.Exp,
+                    bias=negm[:, il : il + 1], scale=1.0, accum_out=rs[:, il : il + 1],
+                )
+            e_sb[u] = eb
+            r_sum[u] = rs
+
+        def stage_e(u):
+            b, h = divmod(u, 2)
+            eb = e_sb[u]
+            blocks = ((0, 0), (2, 1), (3, 2)) if h == 0 else ((0, 0), (1, 1), (2, 2), (3, 3))
+            for dst_blk, src_blk in blocks:
+                nc.tensor.transpose(
+                    out=et[h][:, dst_blk * P : (dst_blk + 1) * P],
+                    in_=eb[:, src_blk * P : (src_blk + 1) * P],
+                    identity=ident_b[:],
+                )
+            g = grouped[2 * (b % 2) + h]
+            first, step = (0, 512) if h == 0 else (1, 513)
+            o_view = (
+                g[:, first : first + 2 * step]
+                .rearrange("p (i x) -> p i x", i=2)[:, :, 0:512]
+                .rearrange("p i (r t) -> p i r t", t=4)[:, :, :, 0:2]
+            )
+            i_view = et[h][:, 0:512].rearrange("p (i t r) -> p i r t", i=2, t=2)
+            nc.scalar.copy(out=o_view, in_=i_view)
+            ec = unit.tile([P, 256], U32, name="ec", align_bytes=64)
+            es = unit.tile([P, 256], U8, name="es", align_bytes=64)
+            nc.vector.quantize_mx(out=ec[:].bitcast(FP8X4), scales=es[:], in_=g[:, 0:1024])
+            e_c[u] = ec
+            e_s[u] = es
+
+        def stage_m(u):
+            b, h = divmod(u, 2)
+            op = ps_o.tile([P, 512], F32, name="op")
+            for il in range(2):
+                cols = slice(il * P, (il + 1) * P)
+                nc.tensor.matmul_mx(
+                    out=op[:, il * 256 : (il + 1) * 256],
+                    lhsT=e_c[u][:, cols].bitcast(FP8X4),
+                    lhsT_scale=e_s[u][:, cols],
+                    rhs=v_c[b][:].bitcast(FP8X4),
+                    rhs_scale=v_s[b][:],
+                    start=True,
+                    stop=True,
+                )
+            rinv = small.tile([P, 2], F32, name="rinv")
+            nc.vector.reciprocal(out=rinv[:], in_=r_sum[u][:])
+            ob = unit.tile([P, 2, 256], F32, name="ob")
+            nc.vector.tensor_tensor(
+                out=ob[:],
+                in0=op[:].rearrange("r (i d) -> r i d", i=2),
+                in1=rinv[:].unsqueeze(2).to_broadcast([P, 2, 256]),
+                op=ALU.mult,
+            )
+            r0 = b * S + h * 256
+            nc.sync.dma_start(
+                out=of[r0 : r0 + 256, :].rearrange("(i p) d -> p i d", p=P), in_=ob[:]
+            )
+
+        stage_t(0)
+        stage_v(0)
+        stage_t(1)
+        stage_s(0)
+        stage_s(1)
+        for j in range(B):
+            if j >= 1:
+                stage_m(2 * j - 2)
+                stage_m(2 * j - 1)
+            if j + 2 < B:
+                stage_t(j + 2)
+            if j + 1 < B:
+                stage_v(j + 1)
+            stage_e(2 * j)
+            stage_e(2 * j + 1)
+            if j + 1 < B:
+                stage_s(2 * j + 2)
+                stage_s(2 * j + 3)
+        stage_m(2 * B - 2)
+        stage_m(2 * B - 1)

@@ -30,7 +30,7 @@ def tile_manualblock_t_kernel(tc, q, k, v, mask, out):
         raw = ctx.enter_context(tc.tile_pool(name="raw", bufs=B))
         tsb = ctx.enter_context(tc.tile_pool(name="tsb", bufs=3))
         vq = ctx.enter_context(tc.tile_pool(name="vq", bufs=4))
-        unit = ctx.enter_context(tc.tile_pool(name="unit", bufs=3))
+        unit = ctx.enter_context(tc.tile_pool(name="unit", bufs=4))
         small = ctx.enter_context(tc.tile_pool(name="small", bufs=6))
         ps_t = ctx.enter_context(tc.psum_pool(name="ps_t", bufs=2))
         ps_s = ctx.enter_context(tc.psum_pool(name="ps_s", bufs=2))
@@ -73,31 +73,35 @@ def tile_manualblock_t_kernel(tc, q, k, v, mask, out):
             et.append(t_)
         nc.tensor.transpose(out=et[0][:, 128:256], in_=zero_b[:], identity=ident_b[:])
 
-        q_t, k_t, v_c, v_s = {}, {}, {}, {}
-        s_ps, e_sb, r_sum, e_c, e_s = {}, {}, {}, {}, {}
+        q_t, k_t, v_g, v_c, v_s = {}, {}, {}, {}, {}
+        s_ps, n_max, e_sb, r_sum, e_c, e_s, o_ps = {}, {}, {}, {}, {}, {}, {}
 
-        def stage_t(b):
-            for which, src, dst in (("k", kraw[b], k_t), ("q", qraw[b], q_t)):
-                words = src[:].bitcast(F32)
-                tp = ps_t.tile([P, 512], F32, name="tp")
-                for t in range(4):
-                    cols = slice(t * P, (t + 1) * P)
-                    nc.tensor.transpose(out=tp[:, cols], in_=words[:, cols], identity=ident_f[:])
-                sb = tsb.tile([P, 512], F32, name=which + "_t")
-                o_view = sb[:].rearrange("w (p t) -> w p t", t=4)
-                i_view = tp[:].rearrange("w (t p) -> w p t", t=4)
-                if which == "k":
-                    nc.vector.tensor_copy(out=o_view, in_=i_view)
-                else:
-                    nc.scalar.copy(out=o_view, in_=i_view)
-                dst[b] = sb
+        def stage_t(which, b):
+            src, dst = (kraw[b], k_t) if which == "k" else (qraw[b], q_t)
+            words = src[:].bitcast(F32)
+            tp = ps_t.tile([P, 512], F32, name="tp")
+            for t in range(4):
+                cols = slice(t * P, (t + 1) * P)
+                nc.tensor.transpose(out=tp[:, cols], in_=words[:, cols], identity=ident_f[:])
+            sb = tsb.tile([P, 512], F32, name=which + "_t")
+            o_view = sb[:].rearrange("w (p t) -> w p t", t=4)
+            i_view = tp[:].rearrange("w (t p) -> w p t", t=4)
+            if which == "k":
+                nc.vector.tensor_copy(out=o_view, in_=i_view)
+            else:
+                nc.scalar.copy(out=o_view, in_=i_view)
+            dst[b] = sb
 
-        def stage_v(b):
+        def stage_vg(b):
             vg = vq.tile([P, 256, 4], BF16, name="vg", align_bytes=64)
             nc.vector.tensor_copy(
                 out=vg[:].rearrange("p (c i) t -> p c t i", i=4),
                 in_=vraw[b][:].rearrange("p t (c i) -> p c t i", i=4),
             )
+            v_g[b] = vg
+
+        def stage_vq(b):
+            vg = v_g[b]
             vc = vq.tile([P, 256], U32, name="vc", align_bytes=64)
             vs = vq.tile([P, 256], U8, name="vs", align_bytes=64)
             nc.vector.quantize_mx(
@@ -129,6 +133,11 @@ def tile_manualblock_t_kernel(tc, q, k, v, mask, out):
                         start=False,
                         stop=(e == 1),
                     )
+            s_ps[u] = sp
+
+        def stage_max(u):
+            h = u % 2
+            sp = s_ps[u]
             negm = small.tile([P, 2], F32, name="negm")
             if h == 0:
                 for il, (i, k0, nk, c0) in enumerate(windows(h)):
@@ -141,6 +150,12 @@ def tile_manualblock_t_kernel(tc, q, k, v, mask, out):
                     out=negm[:], in_=sp[:].rearrange("q (i c) -> q i c", i=2), axis=AX.X,
                     op=ALU.max, negate=True,
                 )
+            n_max[u] = negm
+
+        def stage_exp(u):
+            h = u % 2
+            sp = s_ps[u]
+            negm = n_max[u]
             eb = unit.tile([P, 512], BF16, name="eb")
             rs = small.tile([P, 2], F32, name="rs")
             for il, (i, k0, nk, c0) in enumerate(windows(h)):
@@ -151,7 +166,7 @@ def tile_manualblock_t_kernel(tc, q, k, v, mask, out):
             e_sb[u] = eb
             r_sum[u] = rs
 
-        def stage_e(u):
+        def stage_et(u):
             b, h = divmod(u, 2)
             eb = e_sb[u]
             blocks = ((0, 0), (2, 1), (3, 2)) if h == 0 else ((0, 0), (1, 1), (2, 2), (3, 3))
@@ -161,6 +176,9 @@ def tile_manualblock_t_kernel(tc, q, k, v, mask, out):
                     in_=eb[:, src_blk * P : (src_blk + 1) * P],
                     identity=ident_b[:],
                 )
+
+        def stage_etc(u):
+            b, h = divmod(u, 2)
             g = grouped[2 * (b % 2) + h]
             first, step = (0, 512) if h == 0 else (1, 513)
             o_view = (
@@ -170,13 +188,17 @@ def tile_manualblock_t_kernel(tc, q, k, v, mask, out):
             )
             i_view = et[h][:, 0:512].rearrange("p (i t r) -> p i r t", i=2, t=2)
             nc.scalar.copy(out=o_view, in_=i_view)
+
+        def stage_qe(u):
+            b, h = divmod(u, 2)
+            g = grouped[2 * (b % 2) + h]
             ec = unit.tile([P, 256], U32, name="ec", align_bytes=64)
             es = unit.tile([P, 256], U8, name="es", align_bytes=64)
             nc.vector.quantize_mx(out=ec[:].bitcast(FP8X4), scales=es[:], in_=g[:, 0:1024])
             e_c[u] = ec
             e_s[u] = es
 
-        def stage_m(u):
+        def stage_mx(u):
             b, h = divmod(u, 2)
             op = ps_o.tile([P, 512], F32, name="op")
             for il in range(2):
@@ -190,6 +212,11 @@ def tile_manualblock_t_kernel(tc, q, k, v, mask, out):
                     start=True,
                     stop=True,
                 )
+            o_ps[u] = op
+
+        def stage_out(u):
+            b, h = divmod(u, 2)
+            op = o_ps[u]
             rinv = small.tile([P, 2], F32, name="rinv")
             nc.vector.reciprocal(out=rinv[:], in_=r_sum[u][:])
             ob = unit.tile([P, 2, 256], F32, name="ob")
@@ -204,23 +231,29 @@ def tile_manualblock_t_kernel(tc, q, k, v, mask, out):
                 out=of[r0 : r0 + 256, :].rearrange("(i p) d -> p i d", p=P), in_=ob[:]
             )
 
-        stage_t(0)
-        stage_v(0)
-        stage_t(1)
-        stage_s(0)
-        stage_s(1)
-        for j in range(B):
-            if j >= 1:
-                stage_m(2 * j - 2)
-                stage_m(2 * j - 1)
-            if j + 2 < B:
-                stage_t(j + 2)
-            if j + 1 < B:
-                stage_v(j + 1)
-            stage_e(2 * j)
-            stage_e(2 * j + 1)
-            if j + 1 < B:
-                stage_s(2 * j + 2)
-                stage_s(2 * j + 3)
-        stage_m(2 * B - 2)
-        stage_m(2 * B - 1)
+        units = 2 * B
+        lead = 3
+        with tc.manual_schedule():
+            for n in range(-lead, units + 4):
+                if 0 <= n < units:
+                    stage_s(n)
+                    stage_max(n)
+                x = n + lead
+                if 0 <= x < units:
+                    stage_t("k" if x % 2 == 0 else "q", x // 2)
+                new_v = (n - 1) % 2 == 0 and 0 <= n - 1 < units
+                if new_v:
+                    stage_vg((n - 1) // 2)
+                if 0 <= n - 2 < units:
+                    stage_qe(n - 2)
+                if new_v:
+                    stage_vq((n - 1) // 2)
+                if 0 <= n - 1 < units:
+                    stage_et(n - 1)
+                if 0 <= n - 3 < units:
+                    stage_mx(n - 3)
+                    stage_out(n - 3)
+                if 0 <= n < units:
+                    stage_exp(n)
+                if 0 <= n - 1 < units:
+                    stage_etc(n - 1)

@@ -15,6 +15,7 @@ AX = mybir.AxisListType
 B, S, D = 8, 512, 256
 P = 128
 FLOPS = 4 * B * S * S * D
+SLOT = (0, 2, 1, 3)
 
 
 def tile_manualblock_t_kernel(tc, q, k, v, mask, out):
@@ -60,21 +61,25 @@ def tile_manualblock_t_kernel(tc, q, k, v, mask, out):
         make_identity(nc, ident_f[:])
         ident_b = const.tile([P, P], BF16, name="ident_b")
         make_identity(nc, ident_b[:])
+        spread = []
+        for s in range(2):
+            sp_m = const.tile([P, P, 2], BF16, name="spread%d" % s)
+            nc.vector.memset(sp_m[:], 0.0)
+            nc.vector.tensor_copy(out=sp_m[:, :, s], in_=ident_b[:])
+            spread.append(sp_m)
         zero_b = const.tile([P, P], BF16, name="zero_b")
         nc.vector.memset(zero_b[:], 0.0)
-        grouped = []
-        for n in range(4):
-            g = const.tile([P, 1056], BF16, name="grouped%d" % n, align_bytes=64)
-            nc.vector.memset(g[:], 0.0)
-            grouped.append(g)
         et = []
         for h in range(2):
-            t_ = ps_e.tile([P, 1024], BF16, name="et%d" % h)
+            t_ = ps_e.tile([P, 2, P, 4], BF16, name="et%d" % h)
             et.append(t_)
-        nc.tensor.transpose(out=et[0][:, 128:256], in_=zero_b[:], identity=ident_b[:])
+        for r0 in (0, 64):
+            nc.tensor.transpose(
+                out=et[0][:, 0, r0 : r0 + 64, 2:4], in_=zero_b[:], identity=ident_b[:]
+            )
 
         q_t, k_t, v_g, v_c, v_s = {}, {}, {}, {}, {}
-        s_ps, n_max, e_sb, r_sum, e_c, e_s, o_ps = {}, {}, {}, {}, {}, {}, {}
+        e_g, s_ps, n_max, e_sb, r_sum, e_c, e_s, o_ps = {}, {}, {}, {}, {}, {}, {}, {}
 
         def stage_t(which, b):
             src, dst = (kraw[b], k_t) if which == "k" else (qraw[b], q_t)
@@ -86,17 +91,14 @@ def tile_manualblock_t_kernel(tc, q, k, v, mask, out):
             sb = tsb.tile([P, 512], F32, name=which + "_t")
             o_view = sb[:].rearrange("w (p t) -> w p t", t=4)
             i_view = tp[:].rearrange("w (t p) -> w p t", t=4)
-            if which == "k":
-                nc.vector.tensor_copy(out=o_view, in_=i_view)
-            else:
-                nc.scalar.copy(out=o_view, in_=i_view)
+            nc.scalar.copy(out=o_view, in_=i_view)
             dst[b] = sb
 
         def stage_vg(b):
             vg = vq.tile([P, 256, 4], BF16, name="vg", align_bytes=64)
             nc.vector.tensor_copy(
-                out=vg[:].rearrange("p (c i) t -> p c t i", i=4),
-                in_=vraw[b][:].rearrange("p t (c i) -> p c t i", i=4),
+                out=vg[:].rearrange("p (c i) (y x) -> p c x y i", i=4, y=2),
+                in_=vraw[b][:].rearrange("p (x y) (c i) -> p c x y i", i=4, y=2),
             )
             v_g[b] = vg
 
@@ -167,34 +169,30 @@ def tile_manualblock_t_kernel(tc, q, k, v, mask, out):
             r_sum[u] = rs
 
         def stage_et(u):
-            b, h = divmod(u, 2)
+            h = u % 2
             eb = e_sb[u]
-            blocks = ((0, 0), (2, 1), (3, 2)) if h == 0 else ((0, 0), (1, 1), (2, 2), (3, 3))
-            for dst_blk, src_blk in blocks:
-                nc.tensor.transpose(
-                    out=et[h][:, dst_blk * P : (dst_blk + 1) * P],
-                    in_=eb[:, src_blk * P : (src_blk + 1) * P],
-                    identity=ident_b[:],
-                )
+            for il, (i, k0, nk, c0) in enumerate(windows(h)):
+                for j in range(nk // P):
+                    slot = SLOT[k0 // P + j]
+                    pair = slot // 2
+                    nc.tensor.matmul(
+                        out=et[h][:, il, :, 2 * pair : 2 * pair + 2],
+                        lhsT=eb[:, c0 + j * P : c0 + (j + 1) * P],
+                        rhs=spread[slot % 2][:],
+                        start=True,
+                        stop=True,
+                    )
 
         def stage_etc(u):
-            b, h = divmod(u, 2)
-            g = grouped[2 * (b % 2) + h]
-            first, step = (0, 512) if h == 0 else (1, 513)
-            o_view = (
-                g[:, first : first + 2 * step]
-                .rearrange("p (i x) -> p i x", i=2)[:, :, 0:512]
-                .rearrange("p i (r t) -> p i r t", t=4)[:, :, :, 0:2]
-            )
-            i_view = et[h][:, 0:512].rearrange("p (i t r) -> p i r t", i=2, t=2)
-            nc.scalar.copy(out=o_view, in_=i_view)
+            g = unit.tile([P, 1024], BF16, name="g", align_bytes=64)
+            nc.scalar.copy(out=g[:], in_=et[u % 2][:].rearrange("p i r t -> p (i r t)"))
+            e_g[u] = g
 
         def stage_qe(u):
-            b, h = divmod(u, 2)
-            g = grouped[2 * (b % 2) + h]
+            g = e_g[u]
             ec = unit.tile([P, 256], U32, name="ec", align_bytes=64)
             es = unit.tile([P, 256], U8, name="es", align_bytes=64)
-            nc.vector.quantize_mx(out=ec[:].bitcast(FP8X4), scales=es[:], in_=g[:, 0:1024])
+            nc.vector.quantize_mx(out=ec[:].bitcast(FP8X4), scales=es[:], in_=g[:])
             e_c[u] = ec
             e_s[u] = es
 

@@ -31,8 +31,8 @@ def tile_manualblock_t_kernel(tc, q, k, v, mask, out):
         raw = ctx.enter_context(tc.tile_pool(name="raw", bufs=B))
         tsb = ctx.enter_context(tc.tile_pool(name="tsb", bufs=3))
         vq = ctx.enter_context(tc.tile_pool(name="vq", bufs=4))
-        unit = ctx.enter_context(tc.tile_pool(name="unit", bufs=4))
-        small = ctx.enter_context(tc.tile_pool(name="small", bufs=6))
+        unit = ctx.enter_context(tc.tile_pool(name="unit", bufs=5))
+        small = ctx.enter_context(tc.tile_pool(name="small", bufs=8))
         ps_t = ctx.enter_context(tc.psum_pool(name="ps_t", bufs=2))
         ps_s = ctx.enter_context(tc.psum_pool(name="ps_s", bufs=2))
         ps_e = ctx.enter_context(tc.psum_pool(name="ps_e", bufs=1))
@@ -40,17 +40,26 @@ def tile_manualblock_t_kernel(tc, q, k, v, mask, out):
 
         kraw, qraw, vraw = [], [], []
         mask_sb = const.tile([P, 4, 256], BF16, name="mask_sb")
-        for b in range(B):
+        def load_qk(b):
             rows = slice(b * S, (b + 1) * S)
             kr = raw.tile([P, 1024], BF16, name="kraw")
             nc.sync.dma_start(out=kr[:], in_=kf[rows, :].rearrange("(p t) d -> p (t d)", t=4))
             qr = raw.tile([P, 1024], BF16, name="qraw")
             nc.sync.dma_start(out=qr[:], in_=qf[rows, :].rearrange("(p t) d -> p (t d)", t=4))
-            vr = raw.tile([P, 4, 256], BF16, name="vraw")
-            nc.sync.dma_start(out=vr[:], in_=vf[rows, :].rearrange("(t p) d -> p t d", p=P))
             kraw.append(kr)
             qraw.append(qr)
+
+        def load_v(b):
+            rows = slice(b * S, (b + 1) * S)
+            vr = raw.tile([P, 4, 256], BF16, name="vraw")
+            nc.sync.dma_start(out=vr[:], in_=vf[rows, :].rearrange("(t p) d -> p t d", p=P))
             vraw.append(vr)
+
+        load_qk(0)
+        for b in range(B):
+            if b + 1 < B:
+                load_qk(b + 1)
+            load_v(b)
         nc.scalar.dma_start(out=mask_sb[:, 0, 0:128], in_=mf[0:128, 0:128])
         for i in range(1, 4):
             nc.scalar.dma_start(
@@ -232,7 +241,7 @@ def tile_manualblock_t_kernel(tc, q, k, v, mask, out):
         units = 2 * B
         lead = 3
         with tc.manual_schedule():
-            for n in range(-lead, units + 4):
+            for n in range(-lead, units + 5):
                 if 0 <= n < units:
                     stage_s(n)
                     stage_max(n)
@@ -242,16 +251,16 @@ def tile_manualblock_t_kernel(tc, q, k, v, mask, out):
                 new_v = (n - 1) % 2 == 0 and 0 <= n - 1 < units
                 if new_v:
                     stage_vg((n - 1) // 2)
-                if 0 <= n - 2 < units:
-                    stage_qe(n - 2)
+                if 0 <= n - 3 < units:
+                    stage_qe(n - 3)
                 if new_v:
                     stage_vq((n - 1) // 2)
-                if 0 <= n - 1 < units:
-                    stage_et(n - 1)
-                if 0 <= n - 3 < units:
-                    stage_mx(n - 3)
-                    stage_out(n - 3)
+                if 0 <= n - 2 < units:
+                    stage_et(n - 2)
+                if 0 <= n - 4 < units:
+                    stage_mx(n - 4)
+                    stage_out(n - 4)
                 if 0 <= n < units:
                     stage_exp(n)
-                if 0 <= n - 1 < units:
-                    stage_etc(n - 1)
+                if 0 <= n - 2 < units:
+                    stage_etc(n - 2)

@@ -88,7 +88,7 @@ def tile_manualblock_t_kernel(tc, q, k, v, mask, out):
             )
 
         q_t, k_t, v_g, v_c, v_s = {}, {}, {}, {}, {}
-        e_g, s_ps, n_max, e_sb, r_sum, e_c, e_s, o_ps = {}, {}, {}, {}, {}, {}, {}, {}
+        r_inv, e_g, s_ps, n_max, e_sb, r_sum, e_c, e_s, o_ps = {}, {}, {}, {}, {}, {}, {}, {}, {}
 
         def stage_t(which, b):
             src, dst = (kraw[b], k_t) if which == "k" else (qraw[b], q_t)
@@ -194,7 +194,7 @@ def tile_manualblock_t_kernel(tc, q, k, v, mask, out):
 
         def stage_etc(u):
             g = unit.tile([P, 1024], BF16, name="g", align_bytes=64)
-            nc.scalar.copy(out=g[:], in_=et[u % 2][:].rearrange("p i r t -> p (i r t)"))
+            nc.vector.tensor_copy(out=g[:], in_=et[u % 2][:].rearrange("p i r t -> p (i r t)"))
             e_g[u] = g
 
         def stage_qe(u):
@@ -221,18 +221,20 @@ def tile_manualblock_t_kernel(tc, q, k, v, mask, out):
                 )
             o_ps[u] = op
 
+        def stage_r(u):
+            rinv = small.tile([P, 2], F32, name="rinv")
+            nc.vector.reciprocal(out=rinv[:], in_=r_sum[u][:])
+            r_inv[u] = rinv
+
         def stage_out(u):
             b, h = divmod(u, 2)
             op = o_ps[u]
-            rinv = small.tile([P, 2], F32, name="rinv")
-            nc.vector.reciprocal(out=rinv[:], in_=r_sum[u][:])
             ob = unit.tile([P, 2, 256], F32, name="ob")
-            nc.vector.tensor_tensor(
-                out=ob[:],
-                in0=op[:].rearrange("r (i d) -> r i d", i=2),
-                in1=rinv[:].unsqueeze(2).to_broadcast([P, 2, 256]),
-                op=ALU.mult,
-            )
+            for il in range(2):
+                nc.scalar.activation(
+                    out=ob[:, il, :], in_=op[:, il * 256 : (il + 1) * 256], func=ACT.Copy,
+                    scale=r_inv[u][:, il : il + 1],
+                )
             r0 = b * S + h * 256
             nc.sync.dma_start(
                 out=of[r0 : r0 + 256, :].rearrange("(i p) d -> p i d", p=P), in_=ob[:]
@@ -245,9 +247,13 @@ def tile_manualblock_t_kernel(tc, q, k, v, mask, out):
                 if 0 <= n < units:
                     stage_s(n)
                     stage_max(n)
+                if 0 <= n - 1 < units:
+                    stage_r(n - 1)
                 x = n + lead
                 if 0 <= x < units:
                     stage_t("k" if x % 2 == 0 else "q", x // 2)
+                if 0 <= n < units:
+                    stage_exp(n)
                 new_v = (n - 1) % 2 == 0 and 0 <= n - 1 < units
                 if new_v:
                     stage_vg((n - 1) // 2)
@@ -257,10 +263,7 @@ def tile_manualblock_t_kernel(tc, q, k, v, mask, out):
                     stage_vq((n - 1) // 2)
                 if 0 <= n - 2 < units:
                     stage_et(n - 2)
+                    stage_etc(n - 2)
                 if 0 <= n - 4 < units:
                     stage_mx(n - 4)
                     stage_out(n - 4)
-                if 0 <= n < units:
-                    stage_exp(n)
-                if 0 <= n - 2 < units:
-                    stage_etc(n - 2)

@@ -31,6 +31,7 @@ def tile_manualblock_t_kernel(tc, q, k, v, mask, out):
         raw = ctx.enter_context(tc.tile_pool(name="raw", bufs=B))
         tsb = ctx.enter_context(tc.tile_pool(name="tsb", bufs=3))
         vq = ctx.enter_context(tc.tile_pool(name="vq", bufs=4))
+        vgp = ctx.enter_context(tc.tile_pool(name="vgp", bufs=B))
         unit = ctx.enter_context(tc.tile_pool(name="unit", bufs=5))
         small = ctx.enter_context(tc.tile_pool(name="small", bufs=8))
         ps_t = ctx.enter_context(tc.psum_pool(name="ps_t", bufs=2))
@@ -104,10 +105,14 @@ def tile_manualblock_t_kernel(tc, q, k, v, mask, out):
             dst[b] = sb
 
         def stage_vg(b):
-            vg = vq.tile([P, 256, 4], BF16, name="vg", align_bytes=64)
-            nc.vector.tensor_copy(
-                out=vg[:].rearrange("p (c i) (y x) -> p c x y i", i=4, y=2),
-                in_=vraw[b][:].rearrange("p (x y) (c i) -> p c x y i", i=4, y=2),
+            vg = vgp.tile([P, 256, 4], BF16, name="vg", align_bytes=64)
+            nc.gpsimd.tensor_scalar(
+                out=vg[:].rearrange("p d (y x) -> p d y x", y=2),
+                in0=vraw[b][:].rearrange("p (x y) d -> p d y x", y=2),
+                scalar1=1.0,
+                scalar2=0.0,
+                op0=ALU.mult,
+                op1=ALU.add,
             )
             v_g[b] = vg
 
@@ -243,6 +248,8 @@ def tile_manualblock_t_kernel(tc, q, k, v, mask, out):
         units = 2 * B
         lead = 3
         with tc.manual_schedule():
+            for b in range(B):
+                stage_vg(b)
             for n in range(-lead, units + 5):
                 if 0 <= n < units:
                     stage_s(n)
@@ -255,8 +262,6 @@ def tile_manualblock_t_kernel(tc, q, k, v, mask, out):
                 if 0 <= n < units:
                     stage_exp(n)
                 new_v = (n - 1) % 2 == 0 and 0 <= n - 1 < units
-                if new_v:
-                    stage_vg((n - 1) // 2)
                 if 0 <= n - 3 < units:
                     stage_qe(n - 3)
                 if new_v:

@@ -101,7 +101,10 @@ def tile_manualblock_t_kernel(tc, q, k, v, mask, out):
             sb = tsb.tile([P, 512], F32, name=which + "_t")
             o_view = sb[:].rearrange("w (p t) -> w p t", t=4)
             i_view = tp[:].rearrange("w (t p) -> w p t", t=4)
-            nc.scalar.copy(out=o_view, in_=i_view)
+            if which == "k" and b % 2 == 1:
+                nc.vector.tensor_copy(out=o_view, in_=i_view)
+            else:
+                nc.scalar.copy(out=o_view, in_=i_view)
             dst[b] = sb
 
         def stage_vg(b):
@@ -211,12 +214,18 @@ def tile_manualblock_t_kernel(tc, q, k, v, mask, out):
             e_s[u] = es
 
         def stage_mx(u):
-            b, h = divmod(u, 2)
-            op = ps_o.tile([P, 512], F32, name="op")
+            b = u // 2
+            if u == 2 * B - 1:
+                op = ps_o.tile([P, 512], F32, name="op")
+                tp = ps_t.tile([P, 512], F32, name="tp")
+                dsts = [op[:, 0:256], tp[:, 0:256]]
+            else:
+                op = ps_o.tile([P, 512], F32, name="op")
+                dsts = [op[:, il * 256 : (il + 1) * 256] for il in range(2)]
             for il in range(2):
                 cols = slice(il * P, (il + 1) * P)
                 nc.tensor.matmul_mx(
-                    out=op[:, il * 256 : (il + 1) * 256],
+                    out=dsts[il],
                     lhsT=e_c[u][:, cols].bitcast(FP8X4),
                     lhsT_scale=e_s[u][:, cols],
                     rhs=v_c[b][:].bitcast(FP8X4),
@@ -224,7 +233,7 @@ def tile_manualblock_t_kernel(tc, q, k, v, mask, out):
                     start=True,
                     stop=True,
                 )
-            o_ps[u] = op
+            o_ps[u] = dsts
 
         def stage_r(u):
             rinv = small.tile([P, 2], F32, name="rinv")
@@ -233,17 +242,24 @@ def tile_manualblock_t_kernel(tc, q, k, v, mask, out):
 
         def stage_out(u):
             b, h = divmod(u, 2)
-            op = o_ps[u]
+            last = u == 2 * B - 1
             ob = unit.tile([P, 2, 256], F32, name="ob")
-            for il in range(2):
-                nc.scalar.activation(
-                    out=ob[:, il, :], in_=op[:, il * 256 : (il + 1) * 256], func=ACT.Copy,
-                    scale=r_inv[u][:, il : il + 1],
-                )
             r0 = b * S + h * 256
-            nc.sync.dma_start(
-                out=of[r0 : r0 + 256, :].rearrange("(i p) d -> p i d", p=P), in_=ob[:]
-            )
+            for il in range(2):
+                scale = r_inv[u][:, il : il + 1]
+                if last and il == 1:
+                    nc.vector.tensor_scalar(
+                        out=ob[:, il, :], in0=o_ps[u][il], scalar1=scale, scalar2=None, op0=ALU.mult
+                    )
+                else:
+                    nc.scalar.activation(out=ob[:, il, :], in_=o_ps[u][il], func=ACT.Copy, scale=scale)
+            if last:
+                nc.scalar.dma_start(out=of[r0 : r0 + P, :], in_=ob[:, 0, :])
+                nc.sync.dma_start(out=of[r0 + P : r0 + 2 * P, :], in_=ob[:, 1, :])
+            else:
+                nc.sync.dma_start(
+                    out=of[r0 : r0 + 256, :].rearrange("(i p) d -> p i d", p=P), in_=ob[:]
+                )
 
         units = 2 * B
         lead = 3
@@ -261,11 +277,11 @@ def tile_manualblock_t_kernel(tc, q, k, v, mask, out):
                     stage_t("k" if x % 2 == 0 else "q", x // 2)
                 if 0 <= n < units:
                     stage_exp(n)
-                new_v = (n - 1) % 2 == 0 and 0 <= n - 1 < units
+                v_now = [b for b in range(B) if min(2 * b + 1, b + 5) == n]
                 if 0 <= n - 3 < units:
                     stage_qe(n - 3)
-                if new_v:
-                    stage_vq((n - 1) // 2)
+                for b in v_now:
+                    stage_vq(b)
                 if 0 <= n - 2 < units:
                     stage_et(n - 2)
                     stage_etc(n - 2)

@@ -28,7 +28,7 @@ def tile_manualblock_t_kernel(tc, q, k, v, mask, out):
 
     with ExitStack() as ctx:
         const = ctx.enter_context(tc.tile_pool(name="const", bufs=1))
-        raw = ctx.enter_context(tc.tile_pool(name="raw", bufs=B))
+        raw = ctx.enter_context(tc.tile_pool(name="raw", bufs=2 * B))
         tsb = ctx.enter_context(tc.tile_pool(name="tsb", bufs=3))
         vq = ctx.enter_context(tc.tile_pool(name="vq", bufs=4))
         vgp = ctx.enter_context(tc.tile_pool(name="vgp", bufs=B))
@@ -41,25 +41,27 @@ def tile_manualblock_t_kernel(tc, q, k, v, mask, out):
 
         kraw, qraw, vraw = [], [], []
         mask_sb = const.tile([P, 4, 256], BF16, name="mask_sb")
-        def load_qk(b):
-            rows = slice(b * S, (b + 1) * S)
-            kr = raw.tile([P, 1024], BF16, name="kraw")
-            nc.sync.dma_start(out=kr[:], in_=kf[rows, :].rearrange("(p t) d -> p (t d)", t=4))
-            qr = raw.tile([P, 1024], BF16, name="qraw")
-            nc.sync.dma_start(out=qr[:], in_=qf[rows, :].rearrange("(p t) d -> p (t d)", t=4))
+        def load_qk(u):
+            rows = slice(u * 256, (u + 1) * 256)
+            kr = raw.tile([P, 512], BF16, name="kraw")
+            nc.sync.dma_start(out=kr[:], in_=kf[rows, :].rearrange("(p t) d -> p (t d)", t=2))
+            qr = raw.tile([P, 512], BF16, name="qraw")
+            nc.sync.dma_start(out=qr[:], in_=qf[rows, :].rearrange("(p t) d -> p (t d)", t=2))
             kraw.append(kr)
             qraw.append(qr)
 
         def load_v(b):
             rows = slice(b * S, (b + 1) * S)
-            vr = raw.tile([P, 4, 256], BF16, name="vraw")
+            vr = raw.tile([P, 4, 256], BF16, name="vraw", bufs=B)
             nc.sync.dma_start(out=vr[:], in_=vf[rows, :].rearrange("(t p) d -> p t d", p=P))
             vraw.append(vr)
 
         load_qk(0)
+        load_qk(1)
         for b in range(B):
             if b + 1 < B:
-                load_qk(b + 1)
+                load_qk(2 * b + 2)
+                load_qk(2 * b + 3)
             load_v(b)
         nc.scalar.dma_start(out=mask_sb[:, 0, 0:128], in_=mf[0:128, 0:128])
         for i in range(1, 4):
@@ -88,24 +90,27 @@ def tile_manualblock_t_kernel(tc, q, k, v, mask, out):
                 out=et[0][:, 0, r0 : r0 + 64, 2:4], in_=zero_b[:], identity=ident_b[:]
             )
 
-        q_t, k_t, v_g, v_c, v_s = {}, {}, {}, {}, {}
+        kq_t, v_g, v_c, v_s = {}, {}, {}, {}
         r_inv, e_g, s_ps, n_max, e_sb, r_sum, e_c, e_s, o_ps = {}, {}, {}, {}, {}, {}, {}, {}, {}
 
-        def stage_t(which, b):
-            src, dst = (kraw[b], k_t) if which == "k" else (qraw[b], q_t)
-            words = src[:].bitcast(F32)
+        def stage_t(u):
+            b, h = divmod(u, 2)
             tp = ps_t.tile([P, 512], F32, name="tp")
-            for t in range(4):
-                cols = slice(t * P, (t + 1) * P)
-                nc.tensor.transpose(out=tp[:, cols], in_=words[:, cols], identity=ident_f[:])
-            sb = tsb.tile([P, 512], F32, name=which + "_t")
-            o_view = sb[:].rearrange("w (p t) -> w p t", t=4)
-            i_view = tp[:].rearrange("w (t p) -> w p t", t=4)
-            if which == "k" and b % 2 == 1:
-                nc.vector.tensor_copy(out=o_view, in_=i_view)
-            else:
-                nc.scalar.copy(out=o_view, in_=i_view)
-            dst[b] = sb
+            for x, src in enumerate((kraw[u], qraw[u])):
+                words = src[:].bitcast(F32)
+                for t in range(2):
+                    nc.tensor.transpose(
+                        out=tp[:, (2 * x + t) * P : (2 * x + t + 1) * P],
+                        in_=words[:, t * P : (t + 1) * P],
+                        identity=ident_f[:],
+                    )
+            if h == 0:
+                kq = tsb.tile([P, 2, 512], F32, name="kq")
+                kq_t[b] = kq
+            nc.scalar.copy(
+                out=kq_t[b][:, :, h * 256 : (h + 1) * 256].rearrange("w x (p t) -> w x p t", t=2),
+                in_=tp[:].rearrange("w (x t p) -> w x p t", x=2, t=2),
+            )
 
         def stage_vg(b):
             vg = vgp.tile([P, 256, 4], BF16, name="vg", align_bytes=64)
@@ -136,8 +141,8 @@ def tile_manualblock_t_kernel(tc, q, k, v, mask, out):
 
         def stage_s(u):
             b, h = divmod(u, 2)
-            qb = q_t[b][:].bitcast(BF16).rearrange("w (r e) -> w r e", e=2)
-            kb = k_t[b][:].bitcast(BF16).rearrange("w (r e) -> w r e", e=2)
+            kb = kq_t[b][:, 0, :].bitcast(BF16).rearrange("w (r e) -> w r e", e=2)
+            qb = kq_t[b][:, 1, :].bitcast(BF16).rearrange("w (r e) -> w r e", e=2)
             sp = ps_s.tile([P, 512], F32, name="sp")
             for i, k0, nk, c0 in windows(h):
                 dst = sp[:, c0 : c0 + nk]
@@ -242,27 +247,22 @@ def tile_manualblock_t_kernel(tc, q, k, v, mask, out):
 
         def stage_out(u):
             b, h = divmod(u, 2)
-            last = u == 2 * B - 1
             ob = unit.tile([P, 2, 256], F32, name="ob")
-            r0 = b * S + h * 256
             for il in range(2):
                 scale = r_inv[u][:, il : il + 1]
-                if last and il == 1:
+                if u == 2 * B - 1 and il == 1:
                     nc.vector.tensor_scalar(
                         out=ob[:, il, :], in0=o_ps[u][il], scalar1=scale, scalar2=None, op0=ALU.mult
                     )
                 else:
                     nc.scalar.activation(out=ob[:, il, :], in_=o_ps[u][il], func=ACT.Copy, scale=scale)
-            if last:
-                nc.scalar.dma_start(out=of[r0 : r0 + P, :], in_=ob[:, 0, :])
-                nc.sync.dma_start(out=of[r0 + P : r0 + 2 * P, :], in_=ob[:, 1, :])
-            else:
-                nc.sync.dma_start(
-                    out=of[r0 : r0 + 256, :].rearrange("(i p) d -> p i d", p=P), in_=ob[:]
-                )
+            r0 = b * S + h * 256
+            nc.sync.dma_start(
+                out=of[r0 : r0 + 256, :].rearrange("(i p) d -> p i d", p=P), in_=ob[:]
+            )
 
         units = 2 * B
-        lead = 3
+        lead = 2
         with tc.manual_schedule():
             for b in range(B):
                 stage_vg(b)
@@ -274,7 +274,7 @@ def tile_manualblock_t_kernel(tc, q, k, v, mask, out):
                     stage_r(n - 1)
                 x = n + lead
                 if 0 <= x < units:
-                    stage_t("k" if x % 2 == 0 else "q", x // 2)
+                    stage_t(x)
                 if 0 <= n < units:
                     stage_exp(n)
                 v_now = [b for b in range(B) if min(2 * b + 1, b + 5) == n]

@@ -6,6 +6,7 @@ from concourse.masks import make_identity
 F32 = mybir.dt.float32
 BF16 = mybir.dt.bfloat16
 U32 = mybir.dt.uint32
+I32 = mybir.dt.int32
 U8 = mybir.dt.uint8
 FP8X4 = mybir.dt.float8_e4m3fn_x4
 ACT = mybir.ActivationFunctionType
@@ -15,7 +16,13 @@ AX = mybir.AxisListType
 B, S, D = 8, 512, 256
 P = 128
 FLOPS = 4 * B * S * S * D
-SLOT = (0, 2, 1, 3)
+UNITS = 2 * B
+RING = 3
+
+WINDOWS = (
+    ((0, 0, 128, 0), (1, 0, 256, 128)),
+    ((2, 128, 256, 0), (3, 256, 256, 256)),
+)
 
 
 def tile_manualblock_t_kernel(tc, q, k, v, mask, out):
@@ -28,41 +35,45 @@ def tile_manualblock_t_kernel(tc, q, k, v, mask, out):
 
     with ExitStack() as ctx:
         const = ctx.enter_context(tc.tile_pool(name="const", bufs=1))
-        raw = ctx.enter_context(tc.tile_pool(name="raw", bufs=2 * B))
+        raw = ctx.enter_context(tc.tile_pool(name="raw", bufs=B))
         tsb = ctx.enter_context(tc.tile_pool(name="tsb", bufs=3))
-        vq = ctx.enter_context(tc.tile_pool(name="vq", bufs=4))
-        vgp = ctx.enter_context(tc.tile_pool(name="vgp", bufs=B))
+        vgp = ctx.enter_context(tc.tile_pool(name="vgp", bufs=4))
         unit = ctx.enter_context(tc.tile_pool(name="unit", bufs=5))
         small = ctx.enter_context(tc.tile_pool(name="small", bufs=8))
         ps_t = ctx.enter_context(tc.psum_pool(name="ps_t", bufs=2))
         ps_s = ctx.enter_context(tc.psum_pool(name="ps_s", bufs=2))
-        ps_e = ctx.enter_context(tc.psum_pool(name="ps_e", bufs=1))
+        ps_e = ctx.enter_context(tc.psum_pool(name="ps_e", bufs=2))
         ps_o = ctx.enter_context(tc.psum_pool(name="ps_o", bufs=2))
 
         kraw, qraw, vraw = [], [], []
-        mask_sb = const.tile([P, 4, 256], BF16, name="mask_sb")
-        def load_qk(u):
-            rows = slice(u * 256, (u + 1) * 256)
-            kr = raw.tile([P, 512], BF16, name="kraw")
-            nc.sync.dma_start(out=kr[:], in_=kf[rows, :].rearrange("(p t) d -> p (t d)", t=2))
-            qr = raw.tile([P, 512], BF16, name="qraw")
-            nc.sync.dma_start(out=qr[:], in_=qf[rows, :].rearrange("(p t) d -> p (t d)", t=2))
-            kraw.append(kr)
-            qraw.append(qr)
 
         def load_v(b):
             rows = slice(b * S, (b + 1) * S)
-            vr = raw.tile([P, 4, 256], BF16, name="vraw", bufs=B)
-            nc.sync.dma_start(out=vr[:], in_=vf[rows, :].rearrange("(t p) d -> p t d", p=P))
-            vraw.append(vr)
+            t_ = raw.tile([P, 4, D], BF16, name="vraw")
+            nc.sync.dma_start(out=t_[:], in_=vf[rows, :].rearrange("(p t) d -> p t d", t=4))
+            vraw.append(t_)
 
-        load_qk(0)
-        load_qk(1)
-        for b in range(B):
-            if b + 1 < B:
-                load_qk(2 * b + 2)
-                load_qk(2 * b + 3)
-            load_v(b)
+        def load_half(x, b, c=0, parts=1):
+            n_t = 4 // parts
+            tiles = (kraw, qraw)[x]
+            if c == 0:
+                t_ = raw.tile([P, parts, n_t, D], BF16, name="kraw" if x == 0 else "qraw")
+                tiles.append(t_)
+            rows = slice(b * S + c * n_t * P, b * S + (c + 1) * n_t * P)
+            nc.sync.dma_start(
+                out=tiles[b][:, c], in_=(kf, qf)[x][rows, :].rearrange("(p t) d -> p t d", t=n_t)
+            )
+
+        for c in range(2):
+            for x in range(2):
+                load_half(x, 0, c, 2)
+        load_half(0, 1)
+        load_v(0)
+        load_half(1, 1)
+        load_half(0, 2)
+        load_half(1, 2)
+        load_v(1)
+        mask_sb = const.tile([P, 4, 256], BF16, name="mask_sb")
         nc.scalar.dma_start(out=mask_sb[:, 0, 0:128], in_=mf[0:128, 0:128])
         for i in range(1, 4):
             nc.scalar.dma_start(
@@ -72,79 +83,86 @@ def tile_manualblock_t_kernel(tc, q, k, v, mask, out):
         ident_f = const.tile([P, P], F32, name="ident_f")
         make_identity(nc, ident_f[:])
         ident_b = const.tile([P, P], BF16, name="ident_b")
-        make_identity(nc, ident_b[:])
-        spread = []
-        for s in range(2):
-            sp_m = const.tile([P, P, 2], BF16, name="spread%d" % s)
-            nc.vector.memset(sp_m[:], 0.0)
-            nc.vector.tensor_copy(out=sp_m[:, :, s], in_=ident_b[:])
-            spread.append(sp_m)
-        zero_b = const.tile([P, P], BF16, name="zero_b")
-        nc.vector.memset(zero_b[:], 0.0)
-        et = []
+        nc.vector.tensor_copy(out=ident_b[:], in_=ident_f[:])
+        e_in = []
         for h in range(2):
-            t_ = ps_e.tile([P, 2, P, 4], BF16, name="et%d" % h)
-            et.append(t_)
-        for r0 in (0, 64):
-            nc.tensor.transpose(
-                out=et[0][:, 0, r0 : r0 + 64, 2:4], in_=zero_b[:], identity=ident_b[:]
-            )
+            row = []
+            for r in range(2):
+                t_ = const.tile([P, 2, P, 2], BF16, name="e_in%d%d" % (h, r))
+                if h == 0:
+                    nc.vector.memset(t_[:, :, 96:128, :], 0.0)
+                row.append(t_)
+            e_in.append(row)
+        v_win = []
+        for r in range(RING):
+            t_ = const.tile([P, 4, D], U32, name="v_win%d" % r, align_bytes=64)
+            nc.gpsimd.memset(t_[:].bitcast(I32), 0)
+            v_win.append(t_)
+        v_parts = (((0, 32),), ((0, 64),), ((32, 64), (64, 128)), ((64, 128),))
 
-        kq_t, v_g, v_c, v_s = {}, {}, {}, {}
-        r_inv, e_g, s_ps, n_max, e_sb, r_sum, e_c, e_s, o_ps = {}, {}, {}, {}, {}, {}, {}, {}, {}
+        t_ps, kT, qT, v_g, v_s = {}, {}, {}, {}, {}
+        r_inv, e_g, s_ps, n_max, r_sum, e_c, e_s, o_ps, v_c = {}, {}, {}, {}, {}, {}, {}, {}, {}
 
-        def stage_t(u):
-            b, h = divmod(u, 2)
-            tp = ps_t.tile([P, 512], F32, name="tp")
-            for x, src in enumerate((kraw[u], qraw[u])):
-                words = src[:].bitcast(F32)
-                for t in range(2):
-                    nc.tensor.transpose(
-                        out=tp[:, (2 * x + t) * P : (2 * x + t + 1) * P],
-                        in_=words[:, t * P : (t + 1) * P],
-                        identity=ident_f[:],
-                    )
-            if h == 0:
-                kq = tsb.tile([P, 2, 512], F32, name="kq")
-                kq_t[b] = kq
-            nc.scalar.copy(
-                out=kq_t[b][:, :, h * 256 : (h + 1) * 256].rearrange("w x (p t) -> w x p t", t=2),
-                in_=tp[:].rearrange("w (x t p) -> w x p t", x=2, t=2),
+        def stage_t(m, c=0):
+            b, x = divmod(m, 2)
+            src = (kraw, qraw)[x][b]
+            n_t = src.shape[2]
+            words = src[:].rearrange("p c t d -> p (c t d)").bitcast(F32)
+            tp = ps_t.tile([P, 4, P], F32, name="tp")
+            for t in range(n_t):
+                nc.tensor.transpose(
+                    out=tp[:, t, :],
+                    in_=words[:, (c * n_t + t) * P : (c * n_t + t + 1) * P],
+                    identity=ident_f[:],
+                )
+            t_ps[m] = tp
+
+        def stage_tc(m, c=0):
+            b, x = divmod(m, 2)
+            n_t = kraw[b].shape[2]
+            dsts = (kT, qT)[x]
+            if c == 0:
+                t_ = tsb.tile([P, S], F32, name="kT" if x == 0 else "qT")
+                dsts[b] = t_
+            args = dict(
+                out=dsts[b][:, c * n_t * P : (c + 1) * n_t * P].rearrange("w (p t) -> w p t", t=n_t),
+                in_=t_ps[m][:, 0:n_t, :].rearrange("w t p -> w p t"),
             )
+            if x == 0:
+                nc.scalar.copy(**args)
+            else:
+                nc.vector.tensor_copy(**args)
 
         def stage_vg(b):
-            vg = vgp.tile([P, 256, 4], BF16, name="vg", align_bytes=64)
+            vg = vgp.tile([P, D, 4], BF16, name="vg", align_bytes=64)
             nc.gpsimd.tensor_scalar(
-                out=vg[:].rearrange("p d (y x) -> p d y x", y=2),
-                in0=vraw[b][:].rearrange("p (x y) d -> p d y x", y=2),
-                scalar1=1.0,
-                scalar2=0.0,
-                op0=ALU.mult,
-                op1=ALU.add,
+                out=vg[:], in0=vraw[b][:].rearrange("p t d -> p d t"),
+                scalar1=1.0, scalar2=0.0, op0=ALU.mult, op1=ALU.add,
             )
             v_g[b] = vg
 
         def stage_vq(b):
-            vg = v_g[b]
-            vc = vq.tile([P, 256], U32, name="vc", align_bytes=64)
-            vs = vq.tile([P, 256], U8, name="vs", align_bytes=64)
+            vc = vgp.tile([P, D], U32, name="vc", align_bytes=64)
+            vs = vgp.tile([P, D], U8, name="vs", align_bytes=64)
             nc.vector.quantize_mx(
-                out=vc[:].bitcast(FP8X4), scales=vs[:], in_=vg[:].rearrange("p d t -> p (d t)")
+                out=vc[:].bitcast(FP8X4), scales=vs[:], in_=v_g[b][:].rearrange("p d t -> p (d t)")
             )
             v_c[b] = vc
             v_s[b] = vs
 
-        def windows(h):
-            if h == 0:
-                return ((0, 0, 128, 0), (1, 0, 256, 128))
-            return ((2, 128, 256, 0), (3, 256, 256, 256))
+        def stage_vw(b):
+            for i in range(4):
+                for p0, p1 in v_parts[i]:
+                    nc.sync.dma_start(
+                        out=v_win[b % RING][p0:p1, i, :].bitcast(I32), in_=v_c[b][p0:p1, :].bitcast(I32)
+                    )
 
         def stage_s(u):
             b, h = divmod(u, 2)
-            kb = kq_t[b][:, 0, :].bitcast(BF16).rearrange("w (r e) -> w r e", e=2)
-            qb = kq_t[b][:, 1, :].bitcast(BF16).rearrange("w (r e) -> w r e", e=2)
+            kb = kT[b][:].bitcast(BF16).rearrange("w (r e) -> w r e", e=2)
+            qb = qT[b][:].bitcast(BF16).rearrange("w (r e) -> w r e", e=2)
             sp = ps_s.tile([P, 512], F32, name="sp")
-            for i, k0, nk, c0 in windows(h):
+            for i, k0, nk, c0 in WINDOWS[h]:
                 dst = sp[:, c0 : c0 + nk]
                 nc.tensor.matmul(
                     out=dst, lhsT=ident_b[:], rhs=mask_sb[:, i, 0:nk], start=True, stop=False
@@ -164,7 +182,7 @@ def tile_manualblock_t_kernel(tc, q, k, v, mask, out):
             sp = s_ps[u]
             negm = small.tile([P, 2], F32, name="negm")
             if h == 0:
-                for il, (i, k0, nk, c0) in enumerate(windows(h)):
+                for il, (i, k0, nk, c0) in enumerate(WINDOWS[h]):
                     nc.vector.tensor_reduce(
                         out=negm[:, il : il + 1], in_=sp[:, c0 : c0 + nk], axis=AX.X, op=ALU.max,
                         negate=True,
@@ -177,114 +195,140 @@ def tile_manualblock_t_kernel(tc, q, k, v, mask, out):
             n_max[u] = negm
 
         def stage_exp(u):
-            h = u % 2
-            sp = s_ps[u]
-            negm = n_max[u]
-            eb = unit.tile([P, 512], BF16, name="eb")
-            rs = small.tile([P, 2], F32, name="rs")
-            for il, (i, k0, nk, c0) in enumerate(windows(h)):
+            b, h = divmod(u, 2)
+            if h == 0:
+                rs = small.tile([P, 4], F32, name="rs")
+                r_sum[b] = rs
+            for il, (i, k0, nk, c0) in enumerate(WINDOWS[h]):
                 nc.scalar.activation(
-                    out=eb[:, c0 : c0 + nk], in_=sp[:, c0 : c0 + nk], func=ACT.Exp,
-                    bias=negm[:, il : il + 1], scale=1.0, accum_out=rs[:, il : il + 1],
+                    out=e_in[i % 2][b % 2][:, :, k0 // 4 : (k0 + nk) // 4, :],
+                    in_=s_ps[u][:, c0 : c0 + nk].rearrange("q (p u e) -> q u p e", u=2, e=2),
+                    func=ACT.Exp, bias=n_max[u][:, il : il + 1], scale=1.0,
+                    accum_out=r_sum[b][:, i : i + 1],
                 )
-            e_sb[u] = eb
-            r_sum[u] = rs
 
         def stage_et(u):
-            h = u % 2
-            eb = e_sb[u]
-            for il, (i, k0, nk, c0) in enumerate(windows(h)):
-                for j in range(nk // P):
-                    slot = SLOT[k0 // P + j]
-                    pair = slot // 2
-                    nc.tensor.matmul(
-                        out=et[h][:, il, :, 2 * pair : 2 * pair + 2],
-                        lhsT=eb[:, c0 + j * P : c0 + (j + 1) * P],
-                        rhs=spread[slot % 2][:],
-                        start=True,
-                        stop=True,
-                    )
+            b, h = divmod(u, 2)
+            words = e_in[h][b % 2][:].rearrange("r u p e -> r (u p e)").bitcast(F32)
+            et = ps_e.tile([P, 2, P], F32, name="et")
+            for x in range(2):
+                nc.tensor.transpose(
+                    out=et[:, x, :], in_=words[:, x * P : (x + 1) * P], identity=ident_f[:]
+                )
+            e_g[u] = et
 
         def stage_etc(u):
-            g = unit.tile([P, 1024], BF16, name="g", align_bytes=64)
-            nc.vector.tensor_copy(out=g[:], in_=et[u % 2][:].rearrange("p i r t -> p (i r t)"))
+            g = unit.tile([P, 512], BF16, name="g", align_bytes=64)
+            nc.vector.tensor_copy(
+                out=g[:].bitcast(F32).rearrange("p (r u) -> p r u", u=2),
+                in_=e_g[u][:].rearrange("p u r -> p r u"),
+            )
             e_g[u] = g
 
         def stage_qe(u):
-            g = e_g[u]
-            ec = unit.tile([P, 256], U32, name="ec", align_bytes=64)
-            es = unit.tile([P, 256], U8, name="es", align_bytes=64)
-            nc.vector.quantize_mx(out=ec[:].bitcast(FP8X4), scales=es[:], in_=g[:])
+            ec = unit.tile([P, P], U32, name="ec", align_bytes=64)
+            es = unit.tile([P, P], U8, name="es", align_bytes=64)
+            nc.vector.quantize_mx(out=ec[:].bitcast(FP8X4), scales=es[:], in_=e_g[u][:])
             e_c[u] = ec
             e_s[u] = es
 
         def stage_mx(u):
-            b = u // 2
-            if u == 2 * B - 1:
-                op = ps_o.tile([P, 512], F32, name="op")
-                tp = ps_t.tile([P, 512], F32, name="tp")
-                dsts = [op[:, 0:256], tp[:, 0:256]]
-            else:
-                op = ps_o.tile([P, 512], F32, name="op")
-                dsts = [op[:, il * 256 : (il + 1) * 256] for il in range(2)]
+            b, h = divmod(u, 2)
+            op = ps_o.tile([P, 2, D], F32, name="op")
+            dsts = [op[:, il, :] for il in range(2)]
+            if u == UNITS - 1:
+                tp = ps_t.tile([P, 4, P], F32, name="tp")
+                dsts[1] = tp[:, 0:2, :].rearrange("p a c -> p (a c)")
             for il in range(2):
-                cols = slice(il * P, (il + 1) * P)
                 nc.tensor.matmul_mx(
                     out=dsts[il],
-                    lhsT=e_c[u][:, cols].bitcast(FP8X4),
-                    lhsT_scale=e_s[u][:, cols],
-                    rhs=v_c[b][:].bitcast(FP8X4),
+                    lhsT=e_c[u][:].bitcast(FP8X4),
+                    lhsT_scale=e_s[u][:],
+                    rhs=v_win[b % RING][:, h + 2 * il, :].bitcast(FP8X4),
                     rhs_scale=v_s[b][:],
                     start=True,
                     stop=True,
                 )
             o_ps[u] = dsts
 
-        def stage_r(u):
-            rinv = small.tile([P, 2], F32, name="rinv")
-            nc.vector.reciprocal(out=rinv[:], in_=r_sum[u][:])
-            r_inv[u] = rinv
+        def stage_r(b):
+            rinv = small.tile([P, 4], F32, name="rinv")
+            nc.vector.reciprocal(out=rinv[:], in_=r_sum[b][:])
+            r_inv[b] = rinv
 
-        def stage_out(u):
+        def stage_out(u, split=False):
             b, h = divmod(u, 2)
-            ob = unit.tile([P, 2, 256], F32, name="ob")
+            ob = unit.tile([P, 2, D], F32, name="ob")
+            rows = of[b * S : (b + 1) * S, :].rearrange("(j i p) d -> p i j d", i=2, p=P)
             for il in range(2):
-                scale = r_inv[u][:, il : il + 1]
-                if u == 2 * B - 1 and il == 1:
+                scale = r_inv[b][:, h + 2 * il : h + 2 * il + 1]
+                if split and il == 1:
                     nc.vector.tensor_scalar(
                         out=ob[:, il, :], in0=o_ps[u][il], scalar1=scale, scalar2=None, op0=ALU.mult
                     )
                 else:
                     nc.scalar.activation(out=ob[:, il, :], in_=o_ps[u][il], func=ACT.Copy, scale=scale)
-            r0 = b * S + h * 256
-            nc.sync.dma_start(
-                out=of[r0 : r0 + 256, :].rearrange("(i p) d -> p i d", p=P), in_=ob[:]
-            )
+                if split:
+                    nc.sync.dma_start(out=rows[:, h, il], in_=ob[:, il, :])
+            if not split:
+                nc.sync.dma_start(out=rows[:, h], in_=ob[:])
 
-        units = 2 * B
-        lead = 2
+        live = lambda u: 0 <= u < UNITS
         with tc.manual_schedule():
-            for b in range(B):
-                stage_vg(b)
-            for n in range(-lead, units + 5):
-                if 0 <= n < units:
-                    stage_s(n)
-                    stage_max(n)
-                if 0 <= n - 1 < units:
-                    stage_r(n - 1)
-                x = n + lead
-                if 0 <= x < units:
-                    stage_t(x)
-                if 0 <= n < units:
-                    stage_exp(n)
-                v_now = [b for b in range(B) if min(2 * b + 1, b + 5) == n]
-                if 0 <= n - 3 < units:
+            for c in range(2):
+                for m in range(2):
+                    stage_t(m, c)
+                    stage_tc(m, c)
+            stage_vg(0)
+            for n in range(UNITS):
+                stage_s(n)
+                if n == 0:
+                    stage_t(2)
+                if live(n - 3):
                     stage_qe(n - 3)
-                for b in v_now:
-                    stage_vq(b)
-                if 0 <= n - 2 < units:
+                if live(n + 2):
+                    stage_tc(n + 2)
+                if n % 2 == 0:
+                    b = n // 2
+                    if b + 1 < B:
+                        stage_vg(b + 1)
+                    if b > 0:
+                        stage_vq(b)
+                        stage_vw(b)
+                    if b + 3 < B:
+                        load_half(0, b + 3)
+                        load_half(1, b + 3)
+                    if b + 2 < B:
+                        load_v(b + 2)
+                if live(n - 4):
+                    stage_out(n - 4)
+                if n % 2 == 0 and live(n - 2):
+                    stage_r(n // 2 - 1)
+                stage_max(n)
+                stage_exp(n)
+                if n == 1:
+                    stage_vq(0)
+                    stage_vw(0)
+                if live(n - 2):
                     stage_et(n - 2)
                     stage_etc(n - 2)
-                if 0 <= n - 4 < units:
-                    stage_mx(n - 4)
-                    stage_out(n - 4)
+                if live(n + 3):
+                    stage_t(n + 3)
+                if live(n - 3):
+                    stage_mx(n - 3)
+            u = UNITS - 1
+            stage_r(B - 1)
+            stage_qe(u - 2)
+            stage_et(u - 1)
+            stage_etc(u - 1)
+            stage_et(u)
+            stage_etc(u)
+            stage_mx(u - 2)
+            stage_qe(u - 1)
+            stage_qe(u)
+            stage_out(u - 3)
+            stage_mx(u - 1)
+            stage_mx(u)
+            stage_out(u - 2)
+            stage_out(u - 1)
+            stage_out(u, split=True)

@@ -70,9 +70,11 @@ def tile_manualblock_t_kernel(tc, q, k, v, mask, out):
         load_half(0, 1)
         load_v(0)
         load_half(1, 1)
-        load_half(0, 2)
-        load_half(1, 2)
-        load_v(1)
+        for b in range(2, B):
+            load_half(0, b)
+            load_v(b - 1)
+            load_half(1, b)
+        load_v(B - 1)
         mask_sb = const.tile([P, 4, 256], BF16, name="mask_sb")
         nc.scalar.dma_start(out=mask_sb[:, 0, 0:128], in_=mf[0:128, 0:128])
         for i in range(1, 4):
@@ -95,8 +97,8 @@ def tile_manualblock_t_kernel(tc, q, k, v, mask, out):
             e_in.append(row)
         v_win = []
         for r in range(RING):
-            t_ = const.tile([P, 4, D], U32, name="v_win%d" % r, align_bytes=64)
-            nc.gpsimd.memset(t_[:].bitcast(I32), 0)
+            t_ = const.tile([P, 4, D], U8, name="v_win%d" % r, align_bytes=64)
+            nc.gpsimd.memset(t_[:].rearrange("p i d -> p (i d)").bitcast(I32), 0)
             v_win.append(t_)
         v_parts = (((0, 32),), ((0, 64),), ((32, 64), (64, 128)), ((64, 128),))
 
@@ -153,8 +155,8 @@ def tile_manualblock_t_kernel(tc, q, k, v, mask, out):
         def stage_vw(b):
             for i in range(4):
                 for p0, p1 in v_parts[i]:
-                    nc.sync.dma_start(
-                        out=v_win[b % RING][p0:p1, i, :].bitcast(I32), in_=v_c[b][p0:p1, :].bitcast(I32)
+                    nc.gpsimd.tensor_copy(
+                        out=v_win[b % RING][p0:p1, i, :].bitcast(I32), in_=v_s[b][p0:p1, :].bitcast(I32)
                     )
 
         def stage_s(u):
@@ -244,8 +246,8 @@ def tile_manualblock_t_kernel(tc, q, k, v, mask, out):
                     out=dsts[il],
                     lhsT=e_c[u][:].bitcast(FP8X4),
                     lhsT_scale=e_s[u][:],
-                    rhs=v_win[b % RING][:, h + 2 * il, :].bitcast(FP8X4),
-                    rhs_scale=v_s[b][:],
+                    rhs=v_c[b][:].bitcast(FP8X4),
+                    rhs_scale=v_win[b % RING][:, h + 2 * il, :],
                     start=True,
                     stop=True,
                 )
@@ -295,11 +297,6 @@ def tile_manualblock_t_kernel(tc, q, k, v, mask, out):
                     if b > 0:
                         stage_vq(b)
                         stage_vw(b)
-                    if b + 3 < B:
-                        load_half(0, b + 3)
-                        load_half(1, b + 3)
-                    if b + 2 < B:
-                        load_v(b + 2)
                 if live(n - 4):
                     stage_out(n - 4)
                 if n % 2 == 0 and live(n - 2):

@@ -17,7 +17,6 @@ B, S, D = 8, 512, 256
 P = 128
 FLOPS = 4 * B * S * S * D
 UNITS = 2 * B
-RING = 3
 
 WINDOWS = (
     ((0, 0, 128, 0), (1, 0, 256, 128)),
@@ -37,13 +36,27 @@ def tile_manualblock_t_kernel(tc, q, k, v, mask, out):
         const = ctx.enter_context(tc.tile_pool(name="const", bufs=1))
         raw = ctx.enter_context(tc.tile_pool(name="raw", bufs=B))
         tsb = ctx.enter_context(tc.tile_pool(name="tsb", bufs=3))
-        vgp = ctx.enter_context(tc.tile_pool(name="vgp", bufs=4))
+        vgp = ctx.enter_context(tc.tile_pool(name="vgp", bufs=B))
         unit = ctx.enter_context(tc.tile_pool(name="unit", bufs=5))
         small = ctx.enter_context(tc.tile_pool(name="small", bufs=8))
         ps_t = ctx.enter_context(tc.psum_pool(name="ps_t", bufs=2))
         ps_s = ctx.enter_context(tc.psum_pool(name="ps_s", bufs=2))
         ps_e = ctx.enter_context(tc.psum_pool(name="ps_e", bufs=2))
         ps_o = ctx.enter_context(tc.psum_pool(name="ps_o", bufs=2))
+
+        ctx.enter_context(tc.manual_schedule())
+
+        ident_f = const.tile([P, P], F32, name="ident_f")
+        make_identity(nc, ident_f[:])
+        ident_b = const.tile([P, P], BF16, name="ident_b")
+        nc.vector.tensor_copy(out=ident_b[:], in_=ident_f[:])
+        mask_sb = const.tile([P, 4, 256], BF16, name="mask_sb")
+        nc.scalar.dma_start(out=mask_sb[:, 0, 0:128], in_=mf[0:128, 0:128])
+        for i in range(1, 4):
+            queue = nc.scalar if i == 1 else nc.gpsimd
+            queue.dma_start(
+                out=mask_sb[:, i, :], in_=mf[i * P : (i + 1) * P, (i - 1) * P : (i + 1) * P]
+            )
 
         kraw, qraw, vraw = [], [], []
 
@@ -67,25 +80,11 @@ def tile_manualblock_t_kernel(tc, q, k, v, mask, out):
         for c in range(2):
             for x in range(2):
                 load_half(x, 0, c, 2)
-        load_half(0, 1)
-        load_v(0)
-        load_half(1, 1)
-        for b in range(2, B):
+        for b in range(1, B):
             load_half(0, b)
-            load_v(b - 1)
             load_half(1, b)
+            load_v(b - 1)
         load_v(B - 1)
-        mask_sb = const.tile([P, 4, 256], BF16, name="mask_sb")
-        nc.scalar.dma_start(out=mask_sb[:, 0, 0:128], in_=mf[0:128, 0:128])
-        for i in range(1, 4):
-            nc.scalar.dma_start(
-                out=mask_sb[:, i, :], in_=mf[i * P : (i + 1) * P, (i - 1) * P : (i + 1) * P]
-            )
-
-        ident_f = const.tile([P, P], F32, name="ident_f")
-        make_identity(nc, ident_f[:])
-        ident_b = const.tile([P, P], BF16, name="ident_b")
-        nc.vector.tensor_copy(out=ident_b[:], in_=ident_f[:])
         e_in = []
         for h in range(2):
             row = []
@@ -96,11 +95,10 @@ def tile_manualblock_t_kernel(tc, q, k, v, mask, out):
                 row.append(t_)
             e_in.append(row)
         v_win = []
-        for r in range(RING):
+        for r in range(3):
             t_ = const.tile([P, 4, D], U8, name="v_win%d" % r, align_bytes=64)
             nc.gpsimd.memset(t_[:].rearrange("p i d -> p (i d)").bitcast(I32), 0)
             v_win.append(t_)
-        v_parts = (((0, 32),), ((0, 64),), ((32, 64), (64, 128)), ((64, 128),))
 
         t_ps, kT, qT, v_g, v_s = {}, {}, {}, {}, {}
         r_inv, e_g, s_ps, n_max, r_sum, e_c, e_s, o_ps, v_c = {}, {}, {}, {}, {}, {}, {}, {}, {}
@@ -145,39 +143,40 @@ def tile_manualblock_t_kernel(tc, q, k, v, mask, out):
 
         def stage_vq(b):
             vc = vgp.tile([P, D], U32, name="vc", align_bytes=64)
-            vs = vgp.tile([P, D], U8, name="vs", align_bytes=64)
             nc.vector.quantize_mx(
-                out=vc[:].bitcast(FP8X4), scales=vs[:], in_=v_g[b][:].rearrange("p d t -> p (d t)")
+                out=vc[:].bitcast(FP8X4), scales=v_win[b % 3][:, 2, :],
+                in_=v_g[b][:].rearrange("p d t -> p (d t)"),
             )
             v_c[b] = vc
-            v_s[b] = vs
 
         def stage_vw(b):
-            for i in range(4):
-                for p0, p1 in v_parts[i]:
-                    nc.gpsimd.tensor_copy(
-                        out=v_win[b % RING][p0:p1, i, :].bitcast(I32), in_=v_s[b][p0:p1, :].bitcast(I32)
-                    )
+            win = v_win[b % 3]
+            for i, p0, p1 in ((1, 0, 64), (3, 64, 128), (0, 0, 32)):
+                nc.gpsimd.tensor_copy(
+                    out=win[p0:p1, i, :].bitcast(I32), in_=win[p0:p1, 2, :].bitcast(I32)
+                )
+            nc.gpsimd.memset(win[0:32, 2, :].bitcast(I32), 0)
 
-        def stage_s(u):
+        def stage_s(u, il):
             b, h = divmod(u, 2)
             kb = kT[b][:].bitcast(BF16).rearrange("w (r e) -> w r e", e=2)
             qb = qT[b][:].bitcast(BF16).rearrange("w (r e) -> w r e", e=2)
-            sp = ps_s.tile([P, 512], F32, name="sp")
-            for i, k0, nk, c0 in WINDOWS[h]:
-                dst = sp[:, c0 : c0 + nk]
+            if il == 0:
+                sp = ps_s.tile([P, 512], F32, name="sp")
+                s_ps[u] = sp
+            i, k0, nk, c0 = WINDOWS[h][il]
+            dst = s_ps[u][:, c0 : c0 + nk]
+            nc.tensor.matmul(
+                out=dst, lhsT=ident_b[:], rhs=mask_sb[:, i, 0:nk], start=True, stop=False
+            )
+            for e in range(2):
                 nc.tensor.matmul(
-                    out=dst, lhsT=ident_b[:], rhs=mask_sb[:, i, 0:nk], start=True, stop=False
+                    out=dst,
+                    lhsT=qb[:, i * P : (i + 1) * P, e],
+                    rhs=kb[:, k0 : k0 + nk, e],
+                    start=False,
+                    stop=(e == 1),
                 )
-                for e in range(2):
-                    nc.tensor.matmul(
-                        out=dst,
-                        lhsT=qb[:, i * P : (i + 1) * P, e],
-                        rhs=kb[:, k0 : k0 + nk, e],
-                        start=False,
-                        stop=(e == 1),
-                    )
-            s_ps[u] = sp
 
         def stage_max(u):
             h = u % 2
@@ -247,7 +246,7 @@ def tile_manualblock_t_kernel(tc, q, k, v, mask, out):
                     lhsT=e_c[u][:].bitcast(FP8X4),
                     lhsT_scale=e_s[u][:],
                     rhs=v_c[b][:].bitcast(FP8X4),
-                    rhs_scale=v_win[b % RING][:, h + 2 * il, :],
+                    rhs_scale=v_win[b % 3][:, h + 2 * il, :],
                     start=True,
                     stop=True,
                 )
@@ -258,7 +257,8 @@ def tile_manualblock_t_kernel(tc, q, k, v, mask, out):
             nc.vector.reciprocal(out=rinv[:], in_=r_sum[b][:])
             r_inv[b] = rinv
 
-        def stage_out(u, split=False):
+        def stage_out(u):
+            split = u >= UNITS - 3
             b, h = divmod(u, 2)
             ob = unit.tile([P, 2, D], F32, name="ob")
             rows = of[b * S : (b + 1) * S, :].rearrange("(j i p) d -> p i j d", i=2, p=P)
@@ -275,57 +275,63 @@ def tile_manualblock_t_kernel(tc, q, k, v, mask, out):
             if not split:
                 nc.sync.dma_start(out=rows[:, h], in_=ob[:])
 
-        live = lambda u: 0 <= u < UNITS
-        with tc.manual_schedule():
-            for c in range(2):
-                for m in range(2):
-                    stage_t(m, c)
-                    stage_tc(m, c)
-            stage_vg(0)
-            for n in range(UNITS):
-                stage_s(n)
+        def step(n):
+            tk, tq, vb = (n + 3) // 2, n // 2 + 1, n // 2
+            if n < UNITS:
+                stage_s(n, 0)
+            if 0 <= n - 5 < UNITS:
+                stage_mx(n - 5)
+            if n < UNITS:
+                stage_s(n, 1)
+            if n % 2 == 1 and tk < B:
+                stage_t(2 * tk)
+            if n % 2 == 0 and tq < B:
                 if n == 0:
                     stage_t(2)
-                if live(n - 3):
-                    stage_qe(n - 3)
-                if live(n + 2):
-                    stage_tc(n + 2)
-                if n % 2 == 0:
-                    b = n // 2
-                    if b + 1 < B:
-                        stage_vg(b + 1)
-                    if b > 0:
-                        stage_vq(b)
-                        stage_vw(b)
-                if live(n - 4):
-                    stage_out(n - 4)
-                if n % 2 == 0 and live(n - 2):
-                    stage_r(n // 2 - 1)
+                stage_t(2 * tq + 1)
+            if 0 <= n - 5 < UNITS:
+                stage_out(n - 5)
+            if n < UNITS:
                 stage_max(n)
                 stage_exp(n)
-                if n == 1:
-                    stage_vq(0)
-                    stage_vw(0)
-                if live(n - 2):
-                    stage_et(n - 2)
-                    stage_etc(n - 2)
-                if live(n + 3):
-                    stage_t(n + 3)
-                if live(n - 3):
-                    stage_mx(n - 3)
-            u = UNITS - 1
-            stage_r(B - 1)
-            stage_qe(u - 2)
-            stage_et(u - 1)
-            stage_etc(u - 1)
-            stage_et(u)
-            stage_etc(u)
-            stage_mx(u - 2)
-            stage_qe(u - 1)
-            stage_qe(u)
-            stage_out(u - 3)
-            stage_mx(u - 1)
-            stage_mx(u)
-            stage_out(u - 2)
-            stage_out(u - 1)
-            stage_out(u, split=True)
+            if 0 <= n - 3 < UNITS:
+                stage_qe(n - 3)
+            if n % 2 == 1 and tk < B:
+                stage_tc(2 * tk)
+            if n % 2 == 0 and tq < B:
+                if n == 0:
+                    stage_tc(2)
+                stage_tc(2 * tq + 1)
+                stage_vg(tq)
+            if n % 2 == 1 and vb < B:
+                stage_vq(vb)
+                stage_vw(vb)
+            if n % 2 == 0 and 0 < n <= UNITS:
+                stage_r(vb - 1)
+            if 0 <= n - 2 < UNITS:
+                stage_et(n - 2)
+                stage_etc(n - 2)
+
+        for c in range(2):
+            for m in range(2):
+                stage_t(m, c)
+                stage_tc(m, c)
+        stage_vg(0)
+        for n in range(UNITS):
+            step(n)
+        u = UNITS - 1
+        stage_r(B - 1)
+        stage_et(u - 1)
+        stage_qe(u - 2)
+        stage_etc(u - 1)
+        stage_mx(u - 4)
+        stage_out(u - 4)
+        stage_et(u)
+        stage_etc(u)
+        stage_qe(u - 1)
+        stage_mx(u - 3)
+        stage_out(u - 3)
+        stage_qe(u)
+        for w in range(u - 2, u + 1):
+            stage_mx(w)
+            stage_out(w)

@@ -50,12 +50,15 @@ def tile_manualblock_t_kernel(tc, q, k, v, mask, out):
         make_identity(nc, ident_f[:])
         ident_b = const.tile([P, P], BF16, name="ident_b")
         nc.vector.tensor_copy(out=ident_b[:], in_=ident_f[:])
-        mask_sb = const.tile([P, 4, 256], BF16, name="mask_sb")
-        nc.scalar.dma_start(out=mask_sb[:, 0, 0:128], in_=mf[0:128, 0:128])
-        for i in range(1, 4):
-            queue = nc.scalar if i == 1 else nc.gpsimd
-            queue.dma_start(
-                out=mask_sb[:, i, :], in_=mf[i * P : (i + 1) * P, (i - 1) * P : (i + 1) * P]
+        mask_sb = []
+        for h in range(2):
+            t_ = const.tile([P, 2, 256 + 128 * h], BF16, name="mask%d" % h)
+            mask_sb.append(t_)
+
+        def load_mask(h):
+            nc.sync.dma_start(
+                out=mask_sb[h][:],
+                in_=mf[256 * h : 256 * (h + 1), 128 * h : 256 * (h + 1)].rearrange("(i p) c -> p i c", p=P),
             )
 
         kraw, qraw, vraw = [], [], []
@@ -80,6 +83,7 @@ def tile_manualblock_t_kernel(tc, q, k, v, mask, out):
         for c in range(2):
             for x in range(2):
                 load_half(x, 0, c, 2)
+            load_mask(c)
         for b in range(1, B):
             load_half(0, b)
             load_half(1, b)
@@ -95,12 +99,12 @@ def tile_manualblock_t_kernel(tc, q, k, v, mask, out):
                 row.append(t_)
             e_in.append(row)
         v_win = []
-        for r in range(3):
-            t_ = const.tile([P, 4, D], U8, name="v_win%d" % r, align_bytes=64)
+        for b in range(B):
+            t_ = const.tile([P, 4, D], U8, name="v_win%d" % b, align_bytes=64)
             nc.gpsimd.memset(t_[:].rearrange("p i d -> p (i d)").bitcast(I32), 0)
             v_win.append(t_)
 
-        t_ps, kT, qT, v_g, v_s = {}, {}, {}, {}, {}
+        t_ps, kT, qT, v_g = {}, {}, {}, {}
         r_inv, e_g, s_ps, n_max, r_sum, e_c, e_s, o_ps, v_c = {}, {}, {}, {}, {}, {}, {}, {}, {}
 
         def stage_t(m, c=0):
@@ -128,29 +132,28 @@ def tile_manualblock_t_kernel(tc, q, k, v, mask, out):
                 out=dsts[b][:, c * n_t * P : (c + 1) * n_t * P].rearrange("w (p t) -> w p t", t=n_t),
                 in_=t_ps[m][:, 0:n_t, :].rearrange("w t p -> w p t"),
             )
-            if x == 0:
-                nc.scalar.copy(**args)
-            else:
-                nc.vector.tensor_copy(**args)
+            nc.scalar.copy(**args)
 
-        def stage_vg(b):
-            vg = vgp.tile([P, D, 4], BF16, name="vg", align_bytes=64)
-            nc.gpsimd.tensor_scalar(
-                out=vg[:], in0=vraw[b][:].rearrange("p t d -> p d t"),
-                scalar1=1.0, scalar2=0.0, op0=ALU.mult, op1=ALU.add,
+        def stage_vg(b, c):
+            if c == 0:
+                t_ = vgp.tile([P, D, 4], BF16, name="vg", align_bytes=64)
+                v_g[b] = t_
+            cols = slice(c * 128, (c + 1) * 128)
+            nc.vector.tensor_copy(
+                out=v_g[b][:, cols, :].rearrange("p (c i) t -> p c t i", i=4),
+                in_=vraw[b][:, :, cols].rearrange("p t (c i) -> p c t i", i=4),
             )
-            v_g[b] = vg
 
         def stage_vq(b):
             vc = vgp.tile([P, D], U32, name="vc", align_bytes=64)
             nc.vector.quantize_mx(
-                out=vc[:].bitcast(FP8X4), scales=v_win[b % 3][:, 2, :],
+                out=vc[:].bitcast(FP8X4), scales=v_win[b][:, 2, :],
                 in_=v_g[b][:].rearrange("p d t -> p (d t)"),
             )
             v_c[b] = vc
 
         def stage_vw(b):
-            win = v_win[b % 3]
+            win = v_win[b]
             for i, p0, p1 in ((1, 0, 64), (3, 64, 128), (0, 0, 32)):
                 nc.gpsimd.tensor_copy(
                     out=win[p0:p1, i, :].bitcast(I32), in_=win[p0:p1, 2, :].bitcast(I32)
@@ -167,7 +170,8 @@ def tile_manualblock_t_kernel(tc, q, k, v, mask, out):
             i, k0, nk, c0 = WINDOWS[h][il]
             dst = s_ps[u][:, c0 : c0 + nk]
             nc.tensor.matmul(
-                out=dst, lhsT=ident_b[:], rhs=mask_sb[:, i, 0:nk], start=True, stop=False
+                out=dst, lhsT=ident_b[:], rhs=mask_sb[h][:, il, k0 - 128 * h : k0 - 128 * h + nk],
+                start=True, stop=False
             )
             for e in range(2):
                 nc.tensor.matmul(
@@ -246,7 +250,7 @@ def tile_manualblock_t_kernel(tc, q, k, v, mask, out):
                     lhsT=e_c[u][:].bitcast(FP8X4),
                     lhsT_scale=e_s[u][:],
                     rhs=v_c[b][:].bitcast(FP8X4),
-                    rhs_scale=v_win[b % 3][:, h + 2 * il, :],
+                    rhs_scale=v_win[b][:, h + 2 * il, :],
                     start=True,
                     stop=True,
                 )
@@ -276,62 +280,49 @@ def tile_manualblock_t_kernel(tc, q, k, v, mask, out):
                 nc.sync.dma_start(out=rows[:, h], in_=ob[:])
 
         def step(n):
-            tk, tq, vb = (n + 3) // 2, n // 2 + 1, n // 2
+            b, odd = divmod(n, 2)
             if n < UNITS:
                 stage_s(n, 0)
-            if 0 <= n - 5 < UNITS:
-                stage_mx(n - 5)
-            if n < UNITS:
                 stage_s(n, 1)
-            if n % 2 == 1 and tk < B:
-                stage_t(2 * tk)
-            if n % 2 == 0 and tq < B:
-                if n == 0:
-                    stage_t(2)
-                stage_t(2 * tq + 1)
-            if 0 <= n - 5 < UNITS:
-                stage_out(n - 5)
+            new = []
+            if n == 0:
+                new.append(2)
+            if odd and b + 2 < B:
+                new.append(2 * b + 4)
+            if not odd and b + 1 < B:
+                new.append(2 * b + 3)
+            for m in new:
+                stage_t(m)
             if n < UNITS:
                 stage_max(n)
-                stage_exp(n)
+            for m in new:
+                stage_tc(m)
+            if odd and b + 1 < B:
+                stage_vg(b + 1, 0)
+            if not odd and b < B:
+                if n == 0:
+                    stage_vg(0, 0)
+                stage_vg(b, 1)
+            if not odd and 0 <= b - 1 < B:
+                stage_vq(b - 1)
+                stage_vw(b - 1)
             if 0 <= n - 3 < UNITS:
                 stage_qe(n - 3)
-            if n % 2 == 1 and tk < B:
-                stage_tc(2 * tk)
-            if n % 2 == 0 and tq < B:
-                if n == 0:
-                    stage_tc(2)
-                stage_tc(2 * tq + 1)
-                stage_vg(tq)
-            if n % 2 == 1 and vb < B:
-                stage_vq(vb)
-                stage_vw(vb)
-            if n % 2 == 0 and 0 < n <= UNITS:
-                stage_r(vb - 1)
+            if 0 <= n - 5 < UNITS:
+                stage_mx(n - 5)
+            if not odd and 0 <= b - 1 < B:
+                stage_r(b - 1)
             if 0 <= n - 2 < UNITS:
                 stage_et(n - 2)
                 stage_etc(n - 2)
+            if 0 <= n - 5 < UNITS:
+                stage_out(n - 5)
+            if n < UNITS:
+                stage_exp(n)
 
         for c in range(2):
             for m in range(2):
                 stage_t(m, c)
                 stage_tc(m, c)
-        stage_vg(0)
-        for n in range(UNITS):
+        for n in range(UNITS + 5):
             step(n)
-        u = UNITS - 1
-        stage_r(B - 1)
-        stage_et(u - 1)
-        stage_qe(u - 2)
-        stage_etc(u - 1)
-        stage_mx(u - 4)
-        stage_out(u - 4)
-        stage_et(u)
-        stage_etc(u)
-        stage_qe(u - 1)
-        stage_mx(u - 3)
-        stage_out(u - 3)
-        stage_qe(u)
-        for w in range(u - 2, u + 1):
-            stage_mx(w)
-            stage_out(w)

@@ -46,6 +46,15 @@ def tile_manualblock_t_kernel(tc, q, k, v, mask, out):
 
         ctx.enter_context(tc.manual_schedule())
 
+        warm = const.tile([P, 512], BF16, name="warm")
+        nc.vector.memset(warm[:], 0.0)
+        op = ps_o.tile([P, 2, D], F32, name="op")
+        for w in range(4):
+            nc.tensor.matmul(
+                out=op[:].rearrange("p i d -> p (i d)"), lhsT=warm[:, 0:P], rhs=warm[:],
+                start=True, stop=True,
+            )
+
         ident_f = const.tile([P, P], F32, name="ident_f")
         make_identity(nc, ident_f[:])
         ident_b = const.tile([P, P], BF16, name="ident_b")
@@ -239,11 +248,13 @@ def tile_manualblock_t_kernel(tc, q, k, v, mask, out):
 
         def stage_mx(u):
             b, h = divmod(u, 2)
-            op = ps_o.tile([P, 2, D], F32, name="op")
-            dsts = [op[:, il, :] for il in range(2)]
-            if u == UNITS - 1:
+            if u < UNITS - 2:
+                op = ps_o.tile([P, 2, D], F32, name="op")
+                dsts = [op[:, il, :] for il in range(2)]
+            else:
+                sp = ps_s.tile([P, 512], F32, name="sp")
                 tp = ps_t.tile([P, 4, P], F32, name="tp")
-                dsts[1] = tp[:, 0:2, :].rearrange("p a c -> p (a c)")
+                dsts = [sp[:, 0:D], tp[:, 0:2, :].rearrange("p a c -> p (a c)")]
             for il in range(2):
                 nc.tensor.matmul_mx(
                     out=dsts[il],

@@ -279,7 +279,7 @@ def tile_manualblock_t_kernel(tc, q, k, v, mask, out):
             rows = of[b * S : (b + 1) * S, :].rearrange("(j i p) d -> p i j d", i=2, p=P)
             for il in range(2):
                 scale = r_inv[b][:, h + 2 * il : h + 2 * il + 1]
-                if split and il == 1:
+                if il == 1 and (split or u % 4 == 2):
                     nc.vector.tensor_scalar(
                         out=ob[:, il, :], in0=o_ps[u][il], scalar1=scale, scalar2=None, op0=ALU.mult
                     )

@@ -59,16 +59,19 @@ def tile_manualblock_t_kernel(tc, q, k, v, mask, out):
         make_identity(nc, ident_f[:])
         ident_b = const.tile([P, P], BF16, name="ident_b")
         nc.vector.tensor_copy(out=ident_b[:], in_=ident_f[:])
-        mask_sb = []
-        for h in range(2):
-            t_ = const.tile([P, 2, 256 + 128 * h], BF16, name="mask%d" % h)
-            mask_sb.append(t_)
+        mask_sb = const.tile([P, 4, 256], BF16, name="mask_sb")
 
         def load_mask(h):
-            nc.sync.dma_start(
-                out=mask_sb[h][:],
-                in_=mf[256 * h : 256 * (h + 1), 128 * h : 256 * (h + 1)].rearrange("(i p) c -> p i c", p=P),
-            )
+            if h == 0:
+                nc.sync.dma_start(
+                    out=mask_sb[:, 0:2, :], in_=mf[0:256, 0:256].rearrange("(i p) c -> p i c", p=P)
+                )
+            else:
+                for i in range(2, 4):
+                    nc.sync.dma_start(
+                        out=mask_sb[:, i, :],
+                        in_=mf[i * P : (i + 1) * P, (i - 1) * P : (i + 1) * P],
+                    )
 
         kraw, qraw, vraw = [], [], []
 
@@ -179,7 +182,7 @@ def tile_manualblock_t_kernel(tc, q, k, v, mask, out):
             i, k0, nk, c0 = WINDOWS[h][il]
             dst = s_ps[u][:, c0 : c0 + nk]
             nc.tensor.matmul(
-                out=dst, lhsT=ident_b[:], rhs=mask_sb[h][:, il, k0 - 128 * h : k0 - 128 * h + nk],
+                out=dst, lhsT=ident_b[:], rhs=mask_sb[:, i, 0:nk],
                 start=True, stop=False
             )
             for e in range(2):

from contextlib import ExitStack

import concourse.mybir as mybir
from concourse.masks import make_identity

F32 = mybir.dt.float32
BF16 = mybir.dt.bfloat16
U32 = mybir.dt.uint32
I32 = mybir.dt.int32
U8 = mybir.dt.uint8
FP8X4 = mybir.dt.float8_e4m3fn_x4
ACT = mybir.ActivationFunctionType
ALU = mybir.AluOpType
AX = mybir.AxisListType

B, S, D = 8, 512, 256
P = 128
FLOPS = 4 * B * S * S * D
UNITS = 2 * B

WINDOWS = (
    ((0, 0, 128, 0), (1, 0, 256, 128)),
    ((2, 128, 256, 0), (3, 256, 256, 256)),
)


def tile_manualblock_t_kernel(tc, q, k, v, mask, out):
    nc = tc.nc
    qf = q.flatten_outer_dims()
    kf = k.flatten_outer_dims()
    vf = v.flatten_outer_dims()
    mf = mask.flatten_outer_dims()
    of = out.flatten_outer_dims()

    with ExitStack() as ctx:
        const = ctx.enter_context(tc.tile_pool(name="const", bufs=1))
        raw = ctx.enter_context(tc.tile_pool(name="raw", bufs=B))
        tsb = ctx.enter_context(tc.tile_pool(name="tsb", bufs=3))
        vgp = ctx.enter_context(tc.tile_pool(name="vgp", bufs=B))
        unit = ctx.enter_context(tc.tile_pool(name="unit", bufs=5))
        small = ctx.enter_context(tc.tile_pool(name="small", bufs=8))
        ps_t = ctx.enter_context(tc.psum_pool(name="ps_t", bufs=2))
        ps_s = ctx.enter_context(tc.psum_pool(name="ps_s", bufs=2))
        ps_e = ctx.enter_context(tc.psum_pool(name="ps_e", bufs=2))
        ps_o = ctx.enter_context(tc.psum_pool(name="ps_o", bufs=2))

        ctx.enter_context(tc.manual_schedule())

        warm = const.tile([P, 512], BF16, name="warm")
        nc.vector.memset(warm[:], 0.0)
        op = ps_o.tile([P, 2, D], F32, name="op")
        for w in range(4):
            nc.tensor.matmul(
                out=op[:].rearrange("p i d -> p (i d)"), lhsT=warm[:, 0:P], rhs=warm[:],
                start=True, stop=True,
            )

        ident_f = const.tile([P, P], F32, name="ident_f")
        make_identity(nc, ident_f[:])
        ident_b = const.tile([P, P], BF16, name="ident_b")
        nc.vector.tensor_copy(out=ident_b[:], in_=ident_f[:])
        mask_sb = const.tile([P, 4, 256], BF16, name="mask_sb")

        def load_mask(h):
            if h == 0:
                nc.sync.dma_start(
                    out=mask_sb[:, 0:2, :], in_=mf[0:256, 0:256].rearrange("(i p) c -> p i c", p=P)
                )
            else:
                for i in range(2, 4):
                    nc.sync.dma_start(
                        out=mask_sb[:, i, :],
                        in_=mf[i * P : (i + 1) * P, (i - 1) * P : (i + 1) * P],
                    )

        kraw, qraw, vraw = [], [], []

        def load_v(b):
            rows = slice(b * S, (b + 1) * S)
            t_ = raw.tile([P, 4, D], BF16, name="vraw")
            nc.sync.dma_start(out=t_[:], in_=vf[rows, :].rearrange("(p t) d -> p t d", t=4))
            vraw.append(t_)

        def load_half(x, b, c=0, parts=1):
            n_t = 4 // parts
            tiles = (kraw, qraw)[x]
            if c == 0:
                t_ = raw.tile([P, parts, n_t, D], BF16, name="kraw" if x == 0 else "qraw")
                tiles.append(t_)
            rows = slice(b * S + c * n_t * P, b * S + (c + 1) * n_t * P)
            nc.sync.dma_start(
                out=tiles[b][:, c], in_=(kf, qf)[x][rows, :].rearrange("(p t) d -> p t d", t=n_t)
            )

        for c in range(2):
            for x in range(2):
                load_half(x, 0, c, 2)
            load_mask(c)
        for b in range(1, B):
            load_half(0, b)
            load_half(1, b)
            load_v(b - 1)
        load_v(B - 1)
        e_in = []
        for h in range(2):
            row = []
            for r in range(2):
                t_ = const.tile([P, 2, P, 2], BF16, name="e_in%d%d" % (h, r))
                if h == 0:
                    nc.vector.memset(t_[:, :, 96:128, :], 0.0)
                row.append(t_)
            e_in.append(row)
        v_win = []
        for b in range(B):
            t_ = const.tile([P, 4, D], U8, name="v_win%d" % b, align_bytes=64)
            nc.gpsimd.memset(t_[:].rearrange("p i d -> p (i d)").bitcast(I32), 0)
            v_win.append(t_)

        t_ps, kT, qT, v_g = {}, {}, {}, {}
        r_inv, e_g, s_ps, n_max, r_sum, e_c, e_s, o_ps, v_c = {}, {}, {}, {}, {}, {}, {}, {}, {}

        def stage_t(m, c=0):
            b, x = divmod(m, 2)
            src = (kraw, qraw)[x][b]
            n_t = src.shape[2]
            words = src[:].rearrange("p c t d -> p (c t d)").bitcast(F32)
            tp = ps_t.tile([P, 4, P], F32, name="tp")
            for t in range(n_t):
                nc.tensor.transpose(
                    out=tp[:, t, :],
                    in_=words[:, (c * n_t + t) * P : (c * n_t + t + 1) * P],
                    identity=ident_f[:],
                )
            t_ps[m] = tp

        def stage_tc(m, c=0):
            b, x = divmod(m, 2)
            n_t = kraw[b].shape[2]
            dsts = (kT, qT)[x]
            if c == 0:
                t_ = tsb.tile([P, S], F32, name="kT" if x == 0 else "qT")
                dsts[b] = t_
            args = dict(
                out=dsts[b][:, c * n_t * P : (c + 1) * n_t * P].rearrange("w (p t) -> w p t", t=n_t),
                in_=t_ps[m][:, 0:n_t, :].rearrange("w t p -> w p t"),
            )
            nc.scalar.copy(**args)

        def stage_vg(b, c):
            if c == 0:
                t_ = vgp.tile([P, D, 4], BF16, name="vg", align_bytes=64)
                v_g[b] = t_
            cols = slice(c * 128, (c + 1) * 128)
            nc.vector.tensor_copy(
                out=v_g[b][:, cols, :].rearrange("p (c i) t -> p c t i", i=4),
                in_=vraw[b][:, :, cols].rearrange("p t (c i) -> p c t i", i=4),
            )

        def stage_vq(b):
            vc = vgp.tile([P, D], U32, name="vc", align_bytes=64)
            nc.vector.quantize_mx(
                out=vc[:].bitcast(FP8X4), scales=v_win[b][:, 2, :],
                in_=v_g[b][:].rearrange("p d t -> p (d t)"),
            )
            v_c[b] = vc

        def stage_vw(b):
            win = v_win[b]
            for i, p0, p1 in ((1, 0, 64), (3, 64, 128), (0, 0, 32)):
                nc.gpsimd.tensor_copy(
                    out=win[p0:p1, i, :].bitcast(I32), in_=win[p0:p1, 2, :].bitcast(I32)
                )
            nc.gpsimd.memset(win[0:32, 2, :].bitcast(I32), 0)

        def stage_s(u, il):
            b, h = divmod(u, 2)
            kb = kT[b][:].bitcast(BF16).rearrange("w (r e) -> w r e", e=2)
            qb = qT[b][:].bitcast(BF16).rearrange("w (r e) -> w r e", e=2)
            if il == 0:
                sp = ps_s.tile([P, 512], F32, name="sp")
                s_ps[u] = sp
            i, k0, nk, c0 = WINDOWS[h][il]
            dst = s_ps[u][:, c0 : c0 + nk]
            nc.tensor.matmul(
                out=dst, lhsT=ident_b[:], rhs=mask_sb[:, i, 0:nk],
                start=True, stop=False
            )
            for e in range(2):
                nc.tensor.matmul(
                    out=dst,
                    lhsT=qb[:, i * P : (i + 1) * P, e],
                    rhs=kb[:, k0 : k0 + nk, e],
                    start=False,
                    stop=(e == 1),
                )

        def stage_max(u):
            h = u % 2
            sp = s_ps[u]
            negm = small.tile([P, 2], F32, name="negm")
            if h == 0:
                for il, (i, k0, nk, c0) in enumerate(WINDOWS[h]):
                    nc.vector.tensor_reduce(
                        out=negm[:, il : il + 1], in_=sp[:, c0 : c0 + nk], axis=AX.X, op=ALU.max,
                        negate=True,
                    )
            else:
                nc.vector.tensor_reduce(
                    out=negm[:], in_=sp[:].rearrange("q (i c) -> q i c", i=2), axis=AX.X,
                    op=ALU.max, negate=True,
                )
            n_max[u] = negm

        def stage_exp(u):
            b, h = divmod(u, 2)
            if h == 0:
                rs = small.tile([P, 4], F32, name="rs")
                r_sum[b] = rs
            for il, (i, k0, nk, c0) in enumerate(WINDOWS[h]):
                nc.scalar.activation(
                    out=e_in[i % 2][b % 2][:, :, k0 // 4 : (k0 + nk) // 4, :],
                    in_=s_ps[u][:, c0 : c0 + nk].rearrange("q (p u e) -> q u p e", u=2, e=2),
                    func=ACT.Exp, bias=n_max[u][:, il : il + 1], scale=1.0,
                    accum_out=r_sum[b][:, i : i + 1],
                )

        def stage_et(u):
            b, h = divmod(u, 2)
            words = e_in[h][b % 2][:].rearrange("r u p e -> r (u p e)").bitcast(F32)
            et = ps_e.tile([P, 2, P], F32, name="et")
            for x in range(2):
                nc.tensor.transpose(
                    out=et[:, x, :], in_=words[:, x * P : (x + 1) * P], identity=ident_f[:]
                )
            e_g[u] = et

        def stage_etc(u):
            g = unit.tile([P, 512], BF16, name="g", align_bytes=64)
            nc.vector.tensor_copy(
                out=g[:].bitcast(F32).rearrange("p (r u) -> p r u", u=2),
                in_=e_g[u][:].rearrange("p u r -> p r u"),
            )
            e_g[u] = g

        def stage_qe(u):
            ec = unit.tile([P, P], U32, name="ec", align_bytes=64)
            es = unit.tile([P, P], U8, name="es", align_bytes=64)
            nc.vector.quantize_mx(out=ec[:].bitcast(FP8X4), scales=es[:], in_=e_g[u][:])
            e_c[u] = ec
            e_s[u] = es

        def stage_mx(u):
            b, h = divmod(u, 2)
            if u < UNITS - 2:
                op = ps_o.tile([P, 2, D], F32, name="op")
                dsts = [op[:, il, :] for il in range(2)]
            else:
                sp = ps_s.tile([P, 512], F32, name="sp")
                tp = ps_t.tile([P, 4, P], F32, name="tp")
                dsts = [sp[:, 0:D], tp[:, 0:2, :].rearrange("p a c -> p (a c)")]
            for il in range(2):
                nc.tensor.matmul_mx(
                    out=dsts[il],
                    lhsT=e_c[u][:].bitcast(FP8X4),
                    lhsT_scale=e_s[u][:],
                    rhs=v_c[b][:].bitcast(FP8X4),
                    rhs_scale=v_win[b][:, h + 2 * il, :],
                    start=True,
                    stop=True,
                )
            o_ps[u] = dsts

        def stage_r(b):
            rinv = small.tile([P, 4], F32, name="rinv")
            nc.vector.reciprocal(out=rinv[:], in_=r_sum[b][:])
            r_inv[b] = rinv

        def stage_out(u):
            split = u >= UNITS - 3
            b, h = divmod(u, 2)
            ob = unit.tile([P, 2, D], F32, name="ob")
            rows = of[b * S : (b + 1) * S, :].rearrange("(j i p) d -> p i j d", i=2, p=P)
            for il in range(2):
                scale = r_inv[b][:, h + 2 * il : h + 2 * il + 1]
                if il == 1 and (split or u % 4 == 2):
                    nc.vector.tensor_scalar(
                        out=ob[:, il, :], in0=o_ps[u][il], scalar1=scale, scalar2=None, op0=ALU.mult
                    )
                else:
                    nc.scalar.activation(out=ob[:, il, :], in_=o_ps[u][il], func=ACT.Copy, scale=scale)
                if split:
                    nc.sync.dma_start(out=rows[:, h, il], in_=ob[:, il, :])
            if not split:
                nc.sync.dma_start(out=rows[:, h], in_=ob[:])

        def step(n):
            b, odd = divmod(n, 2)
            if n < UNITS:
                stage_s(n, 0)
                stage_s(n, 1)
            new = []
            if n == 0:
                new.append(2)
            if odd and b + 2 < B:
                new.append(2 * b + 4)
            if not odd and b + 1 < B:
                new.append(2 * b + 3)
            for m in new:
                stage_t(m)
            if n < UNITS:
                stage_max(n)
            for m in new:
                stage_tc(m)
            if odd and b + 1 < B:
                stage_vg(b + 1, 0)
            if not odd and b < B:
                if n == 0:
                    stage_vg(0, 0)
                stage_vg(b, 1)
            if not odd and 0 <= b - 1 < B:
                stage_vq(b - 1)
                stage_vw(b - 1)
            if 0 <= n - 3 < UNITS:
                stage_qe(n - 3)
            if 0 <= n - 5 < UNITS:
                stage_mx(n - 5)
            if not odd and 0 <= b - 1 < B:
                stage_r(b - 1)
            if 0 <= n - 2 < UNITS:
                stage_et(n - 2)
                stage_etc(n - 2)
            if 0 <= n - 5 < UNITS:
                stage_out(n - 5)
            if n < UNITS:
                stage_exp(n)

        for c in range(2):
            for m in range(2):
                stage_t(m, c)
                stage_tc(m, c)
        for n in range(UNITS + 5):
            step(n)
